import numpy as np
import ml_dtypes


def mxq(x, axis, fmt="e4m3"):
    dtype, down = {"e4m3": (ml_dtypes.float8_e4m3fn, 7), "e5m2": (ml_dtypes.float8_e5m2, 14)}[fmt]
    v = np.moveaxis(np.asarray(x, np.float32).astype(ml_dtypes.bfloat16).astype(np.float64), axis, -1)
    blocks = v.reshape(v.shape[:-1] + (-1, 32))
    amax = np.abs(blocks).max(-1, keepdims=True)
    byte = np.maximum(np.where(amax > 0, np.frexp(amax)[1] - 1 + 127, 0) - down, 1)
    scale = np.exp2(byte - 127.0)
    codes = (blocks / scale).astype(np.float32).astype(dtype).astype(np.float64)
    return np.moveaxis((codes * scale).reshape(v.shape), -1, axis)


WIDE = False


def mx_kscale(k):
    if not WIDE:
        return np.ones(k)
    levels = np.array([10, -10, 5, -5, 0])
    a = np.random.permutation(np.resize(levels, k // 512 * 4)).reshape(k // 512, 4)
    idx = np.arange(k)
    return np.exp2(a[idx // 512, idx % 128 // 32])


BF16 = ml_dtypes.bfloat16


def bf(x):
    return np.asarray(x, np.float32).astype(BF16)


def f64(x):
    return np.asarray(x).astype(np.float64)


B, P, C, HS, NG = 2, 512, 768, 512, 8
GMIN, GMAX = -1.0, 1.0


def silu(v):
    return v / (1.0 + np.exp(-v))


def rbf(v):
    grid = np.linspace(GMIN, GMAX, NG)
    denom = (GMAX - GMIN) / (NG - 1)
    return np.exp(-np.square((v[..., None] - grid) / denom))


def setup_inputs():
    s = mx_kscale(P * NG)[::NG]
    u = s / s.max()
    r = np.sqrt(np.log(1.0 / u))
    d = (GMAX - GMIN) / (NG - 1)
    m = (GMAX + d * r) * (r > 0)
    return {"x": bf(np.random.standard_normal((B, P, C)) * (d / (d + 2.0 * r))[:, None] + m[:, None]),
            "fc1_spline_w": bf(np.random.standard_normal((HS, P * NG)) * 0.7 / np.sqrt(P) / np.repeat(u, NG)),
            "fc1_base_w": bf(np.random.standard_normal((HS, P)) / np.sqrt(P) / (1.0 + m)),
            "fc1_base_b": bf(np.random.standard_normal(HS) * 0.1)}


def reference(x, fc1_spline_w, fc1_base_w, fc1_base_b):
    h = np.swapaxes(f64(x), 1, 2)
    basis = rbf(h).reshape(B, C, P * NG)
    out = mxq(basis, 2, "e4m3") @ mxq(f64(fc1_spline_w).T, 0, "e4m3")
    out = out + (mxq(silu(h), 2, "e4m3") @ mxq(f64(fc1_base_w).T, 0, "e4m3")) + f64(fc1_base_b)
    return out

@@ -1,0 +1,213 @@
+from contextlib import ExitStack
+
+import concourse.mybir as mybir
+from concourse.masks import make_identity
+
+F32 = mybir.dt.float32
+BF16 = mybir.dt.bfloat16
+U32 = mybir.dt.uint32
+U8 = mybir.dt.uint8
+FP8X4 = mybir.dt.float8_e4m3fn_x4
+ACT = mybir.ActivationFunctionType
+ALU = mybir.AluOpType
+
+P = 128
+PACK = 4
+K_PASS = P * PACK
+BATCH, PATCHES, CHANNELS, OUT_F, CENTRES = 2, 512, 768, 512, 8
+COLS = BATCH * CHANNELS
+ROUND_COLS = 512
+ROUNDS = COLS // ROUND_COLS
+M_TILES = ROUND_COLS // P
+SPLINE_PASSES = PATCHES * CENTRES // K_PASS
+BASE = SPLINE_PASSES
+PATCHES_PER_PASS = K_PASS // CENTRES
+RUN = 4
+
+FLOPS = 2 * COLS * OUT_F * (PATCHES * CENTRES + PATCHES)
+
+
+def tile_kan1_pa_kernel(tc, x, fc1_spline_w, fc1_base_w, fc1_base_b, out):
+    nc = tc.nc
+    out_rows = out.flatten_outer_dims()
+
+    with ExitStack() as ctx:
+        keep = ctx.enter_context(tc.tile_pool(name="keep", bufs=1))
+        shifted_pool = ctx.enter_context(tc.tile_pool(name="shifted", bufs=2))
+        arg_pool = ctx.enter_context(tc.tile_pool(name="arg", bufs=4))
+        grouped_pool = ctx.enter_context(tc.tile_pool(name="grouped", bufs=3))
+        operand_pool = ctx.enter_context(tc.tile_pool(name="operand", bufs=4))
+        w_grouped_pool = ctx.enter_context(tc.tile_pool(name="w_grouped", bufs=2))
+        result_pool = ctx.enter_context(tc.tile_pool(name="result", bufs=4))
+        psum_acc = ctx.enter_context(tc.psum_pool(name="psum_acc", bufs=M_TILES))
+        psum_wt = ctx.enter_context(tc.psum_pool(name="psum_wt", bufs=4))
+
+        ident = keep.tile([P, P], F32)
+        make_identity(nc, ident[:])
+        odd = keep.tile([P, 1], F32)
+        nc.vector.reduce_sum(out=odd[:], in_=ident[:, 1:P:2], axis=mybir.AxisListType.X)
+        pair_mid = keep.tile([P, 2], F32)
+        for u in range(2):
+            nc.vector.tensor_scalar(
+                out=pair_mid[:, u : u + 1], in0=odd[:], scalar1=4.0, scalar2=2.0 * u - 3.0, op0=ALU.mult, op1=ALU.add
+            )
+        neg_centre = keep.tile([P, PACK], F32)
+        for t in range(PACK):
+            nc.vector.tensor_scalar(
+                out=neg_centre[:, t : t + 1], in0=odd[:], scalar1=-4.0, scalar2=3.5 - t, op0=ALU.mult, op1=ALU.add
+            )
+        bias_rows = keep.tile([P, OUT_F], BF16)
+        nc.gpsimd.dma_start(out=bias_rows[:], in_=fc1_base_b.partition_broadcast(P))
+
+        x_twice = [keep.tile([P, 2, COLS], BF16, name="x_twice%d" % h) for h in range(SPLINE_PASSES // 2)]
+        x_four = [keep.tile([P, PACK, CHANNELS], BF16, name="x_four%d" % b) for b in range(BATCH)]
+        w_raw = [keep.tile([P, PACK * K_PASS], BF16, name="w_raw%d" % w) for w in range(SPLINE_PASSES + 1)]
+
+        def load_x_twice(h):
+            for b in range(BATCH):
+                rows = x[b, 2 * PATCHES_PER_PASS * h : 2 * PATCHES_PER_PASS * (h + 1), :]
+                for parity in range(2):
+                    nc.sync.dma_start(
+                        out=x_twice[h][parity:P:2, :, b * CHANNELS : (b + 1) * CHANNELS],
+                        in_=rows.rearrange("(g a) c -> a g c", a=PATCHES_PER_PASS),
+                    )
+
+        def load_weights(w):
+            source = fc1_base_w if w == BASE else fc1_spline_w[:, w * K_PASS : (w + 1) * K_PASS]
+            nc.sync.dma_start(
+                out=w_raw[w][:].rearrange("p (ot k) -> p ot k", k=K_PASS),
+                in_=source.rearrange("(ot p) k -> p ot k", p=P),
+            )
+
+        load_x_twice(0)
+        for b in range(BATCH):
+            nc.sync.dma_start(out=x_four[b][:], in_=x[b].rearrange("(q t) c -> q t c", t=PACK))
+        load_weights(BASE)
+        for h in range(SPLINE_PASSES // 2):
+            if h > 0:
+                load_x_twice(h)
+            load_weights(2 * h)
+            load_weights(2 * h + 1)
+
+        silu_grouped = keep.tile([P, COLS, PACK], BF16, align_bytes=64)
+        silu_codes = keep.tile([P, COLS], U32, align_bytes=64)
+        silu_scales = keep.tile([P, COLS], U8, align_bytes=64)
+        for b in range(BATCH):
+            nc.scalar.activation(
+                out=silu_grouped[:, b * CHANNELS : (b + 1) * CHANNELS, :].rearrange("p (c i) t -> p c t i", i=RUN),
+                in_=x_four[b][:].rearrange("p t (c i) -> p c t i", i=RUN),
+                func=ACT.Silu,
+            )
+        for r in range(ROUNDS):
+            cols = slice(r * ROUND_COLS, (r + 1) * ROUND_COLS)
+            nc.vector.quantize_mx(
+                out=silu_codes[:, cols].bitcast(FP8X4),
+                scales=silu_scales[:, cols],
+                in_=silu_grouped[:, cols, :].rearrange("p c t -> p (c t)"),
+            )
+
+        w_codes = keep.tile([P, SPLINE_PASSES + 1, OUT_F], U32, align_bytes=64)
+        w_scales = keep.tile([P, SPLINE_PASSES + 1, OUT_F], U8, align_bytes=64)
+
+        def prepare_weights(w):
+            words = w_raw[w][:].bitcast(F32)
+            w_grouped = w_grouped_pool.tile([P, OUT_F * PACK], BF16, align_bytes=64)
+            grouped_words = w_grouped[:].bitcast(F32)
+            for half in range(2):
+                wt = psum_wt.tile([P, 2, 2 * P], F32)
+                for o_local in range(2):
+                    first = (2 * half + o_local) * (K_PASS // 2)
+                    for u in range(2):
+                        nc.tensor.transpose(
+                            wt[:, u, o_local * P : (o_local + 1) * P],
+                            words[:, first + u : first + K_PASS // 2 : 2],
+                            ident[:],
+                        )
+                nc.scalar.copy(
+                    out=grouped_words[:, half * 4 * P : (half + 1) * 4 * P].rearrange("p (o u) -> p o u", u=2),
+                    in_=wt[:].rearrange("p u o -> p o u"),
+                )
+            nc.vector.quantize_mx(out=w_codes[:, w, :].bitcast(FP8X4), scales=w_scales[:, w, :], in_=w_grouped[:])
+
+        def basis_operand(r, g):
+            cols = slice(r * ROUND_COLS, (r + 1) * ROUND_COLS)
+            x_rows = x_twice[g // 2][:, g % 2, cols]
+            arg = arg_pool.tile([P, PACK, ROUND_COLS], F32)
+            if g % 4 == 3:
+                for t in range(PACK):
+                    nc.scalar.activation(
+                        out=arg[:, t, :], in_=x_rows, func=ACT.Square, bias=neg_centre[:, t : t + 1], scale=3.5
+                    )
+                exp_bias = 0.0
+            else:
+                shifted = shifted_pool.tile([P, 2, ROUND_COLS], F32)
+                for u in range(2):
+                    nc.vector.tensor_scalar(
+                        out=shifted[:, u, :],
+                        in0=x_rows,
+                        scalar1=3.5,
+                        scalar2=pair_mid[:, u : u + 1],
+                        op0=ALU.mult,
+                        op1=ALU.subtract,
+                    )
+                arg_by_e = arg[:].rearrange("p (u e) c -> p e u c", e=2)
+                for e in range(2):
+                    nc.vector.scalar_tensor_tensor(
+                        out=arg_by_e[:, e, :, :],
+                        in0=shifted[:],
+                        scalar=2.0 * e - 1.0,
+                        in1=shifted[:],
+                        op0=ALU.subtract,
+                        op1=ALU.mult,
+                    )
+                exp_bias = -0.25
+            grouped = grouped_pool.tile([P, ROUND_COLS, PACK], BF16, align_bytes=64)
+            nc.scalar.activation(
+                out=grouped[:].rearrange("p (c i) t -> p c t i", i=RUN),
+                in_=arg[:].rearrange("p t (c i) -> p c t i", i=RUN),
+                func=ACT.Exp,
+                bias=exp_bias,
+                scale=-1.0,
+            )
+            codes = operand_pool.tile([P, ROUND_COLS], U32, align_bytes=64)
+            scales = operand_pool.tile([P, ROUND_COLS], U8, align_bytes=64)
+            nc.vector.quantize_mx(
+                out=codes[:].bitcast(FP8X4), scales=scales[:], in_=grouped[:].rearrange("p c t -> p (c t)")
+            )
+            return codes, scales
+
+        for r in range(ROUNDS):
+            acc = [psum_acc.tile([P, OUT_F], F32, name="acc", tag="acc") for j in range(M_TILES)]
+            if r == 0:
+                prepare_weights(BASE)
+            for j in range(M_TILES):
+                m_cols = slice(r * ROUND_COLS + j * P, r * ROUND_COLS + (j + 1) * P)
+                nc.tensor.matmul_mx(
+                    out=acc[j][:],
+                    lhsT=silu_codes[:, m_cols].bitcast(FP8X4),
+                    lhsT_scale=silu_scales[:, m_cols],
+                    rhs=w_codes[:, BASE, :].bitcast(FP8X4),
+                    rhs_scale=w_scales[:, BASE, :],
+                    start=True,
+                    stop=False,
+                )
+            for g in range(SPLINE_PASSES):
+                if r == 0:
+                    prepare_weights(g)
+                codes, scales = basis_operand(r, g)
+                for j in range(M_TILES):
+                    m_cols = slice(j * P, (j + 1) * P)
+                    nc.tensor.matmul_mx(
+                        out=acc[j][:],
+                        lhsT=codes[:, m_cols].bitcast(FP8X4),
+                        lhsT_scale=scales[:, m_cols],
+                        rhs=w_codes[:, g, :].bitcast(FP8X4),
+                        rhs_scale=w_scales[:, g, :],
+                        start=False,
+                        stop=(g == SPLINE_PASSES - 1),
+                    )
+            for j in range(M_TILES):
+                result = result_pool.tile([P, OUT_F], F32)
+                nc.vector.tensor_tensor(out=result[:], in0=acc[j][:], in1=bias_rows[:], op=ALU.add)
+                first_row = r * ROUND_COLS + j * P
+                nc.sync.dma_start(out=out_rows[first_row : first_row + P, :], in_=result[:])

@@ -20,11 +20,18 @@ ROUND_COLS = 512
 ROUNDS = COLS // ROUND_COLS
 M_TILES = ROUND_COLS // P
 SPLINE_PASSES = PATCHES * CENTRES // K_PASS
+STEPS = ROUNDS * SPLINE_PASSES
 BASE = SPLINE_PASSES
 PATCHES_PER_PASS = K_PASS // CENTRES
+PASSES_PER_LOAD = 2
 RUN = 4
+LEAD = 4
 
 FLOPS = 2 * COLS * OUT_F * (PATCHES * CENTRES + PATCHES)
+
+
+def squared_on_scalar(r, g):
+    return (r == 0 and g == 0) or (r > 0 and g % 3 == 2)
 
 
 def tile_kan1_pa_kernel(tc, x, fc1_spline_w, fc1_base_w, fc1_base_b, out):
@@ -32,12 +39,13 @@ def tile_kan1_pa_kernel(tc, x, fc1_spline_w, fc1_base_w, fc1_base_b, out):
     out_rows = out.flatten_outer_dims()
 
     with ExitStack() as ctx:
+        pass
         keep = ctx.enter_context(tc.tile_pool(name="keep", bufs=1))
-        shifted_pool = ctx.enter_context(tc.tile_pool(name="shifted", bufs=2))
-        arg_pool = ctx.enter_context(tc.tile_pool(name="arg", bufs=4))
-        grouped_pool = ctx.enter_context(tc.tile_pool(name="grouped", bufs=3))
+        shifted_pool = ctx.enter_context(tc.tile_pool(name="shifted", bufs=3))
+        arg_pool = ctx.enter_context(tc.tile_pool(name="arg", bufs=LEAD + 1))
+        grouped_pool = ctx.enter_context(tc.tile_pool(name="grouped", bufs=4))
         operand_pool = ctx.enter_context(tc.tile_pool(name="operand", bufs=4))
-        w_grouped_pool = ctx.enter_context(tc.tile_pool(name="w_grouped", bufs=2))
+        w_grouped_pool = ctx.enter_context(tc.tile_pool(name="w_grouped", bufs=4))
         result_pool = ctx.enter_context(tc.tile_pool(name="result", bufs=4))
         psum_acc = ctx.enter_context(tc.psum_pool(name="psum_acc", bufs=M_TILES))
         psum_wt = ctx.enter_context(tc.psum_pool(name="psum_wt", bufs=4))
@@ -57,20 +65,39 @@ def tile_kan1_pa_kernel(tc, x, fc1_spline_w, fc1_base_w, fc1_base_b, out):
                 out=neg_centre[:, t : t + 1], in0=odd[:], scalar1=-4.0, scalar2=3.5 - t, op0=ALU.mult, op1=ALU.add
             )
         bias_rows = keep.tile([P, OUT_F], BF16)
-        nc.gpsimd.dma_start(out=bias_rows[:], in_=fc1_base_b.partition_broadcast(P))
 
-        x_twice = [keep.tile([P, 2, COLS], BF16, name="x_twice%d" % h) for h in range(SPLINE_PASSES // 2)]
-        x_four = [keep.tile([P, PACK, CHANNELS], BF16, name="x_four%d" % b) for b in range(BATCH)]
+        loads_per_round = SPLINE_PASSES // PASSES_PER_LOAD
+        x_twice = [
+            [keep.tile([P, PASSES_PER_LOAD, ROUND_COLS], BF16, name="x_twice%d_%d" % (r, h)) for h in range(loads_per_round)]
+            for r in range(ROUNDS)
+        ]
+        x_four = [keep.tile([P, PACK, ROUND_COLS], BF16, name="x_four%d" % r) for r in range(ROUNDS)]
         w_raw = [keep.tile([P, PACK * K_PASS], BF16, name="w_raw%d" % w) for w in range(SPLINE_PASSES + 1)]
 
-        def load_x_twice(h):
+        def column_pieces(r):
+            pieces = []
             for b in range(BATCH):
-                rows = x[b, 2 * PATCHES_PER_PASS * h : 2 * PATCHES_PER_PASS * (h + 1), :]
+                lo = max(r * ROUND_COLS, b * CHANNELS)
+                hi = min((r + 1) * ROUND_COLS, (b + 1) * CHANNELS)
+                if lo < hi:
+                    pieces.append((b, lo - b * CHANNELS, hi - b * CHANNELS, lo - r * ROUND_COLS))
+            return pieces
+
+        def load_x_twice(r, h):
+            patches = slice(PASSES_PER_LOAD * PATCHES_PER_PASS * h, PASSES_PER_LOAD * PATCHES_PER_PASS * (h + 1))
+            for b, c_lo, c_hi, col in column_pieces(r):
                 for parity in range(2):
                     nc.sync.dma_start(
-                        out=x_twice[h][parity:P:2, :, b * CHANNELS : (b + 1) * CHANNELS],
-                        in_=rows.rearrange("(g a) c -> a g c", a=PATCHES_PER_PASS),
+                        out=x_twice[r][h][parity:P:2, :, col : col + c_hi - c_lo],
+                        in_=x[b, patches, c_lo:c_hi].rearrange("(g a) c -> a g c", a=PATCHES_PER_PASS),
                     )
+
+        def load_x_four(r):
+            for b, c_lo, c_hi, col in column_pieces(r):
+                nc.sync.dma_start(
+                    out=x_four[r][:, :, col : col + c_hi - c_lo],
+                    in_=x[b, :, c_lo:c_hi].rearrange("(q t) c -> q t c", t=PACK),
+                )
 
         def load_weights(w):
             source = fc1_base_w if w == BASE else fc1_spline_w[:, w * K_PASS : (w + 1) * K_PASS]
@@ -79,42 +106,49 @@ def tile_kan1_pa_kernel(tc, x, fc1_spline_w, fc1_base_w, fc1_base_b, out):
                 in_=source.rearrange("(ot p) k -> p ot k", p=P),
             )
 
-        load_x_twice(0)
-        for b in range(BATCH):
-            nc.sync.dma_start(out=x_four[b][:], in_=x[b].rearrange("(q t) c -> q t c", t=PACK))
+        load_x_twice(0, 0)
+        load_x_four(0)
+        load_x_twice(0, 1)
         load_weights(BASE)
-        for h in range(SPLINE_PASSES // 2):
-            if h > 0:
-                load_x_twice(h)
-            load_weights(2 * h)
-            load_weights(2 * h + 1)
+        load_x_four(1)
+        load_x_four(2)
+        load_x_twice(0, 2)
+        load_weights(0)
+        load_weights(1)
+        load_x_twice(0, 3)
+        for w in range(2, SPLINE_PASSES):
+            load_weights(w)
+        for r in range(1, ROUNDS):
+            for h in range(loads_per_round):
+                load_x_twice(r, h)
+        nc.sync.dma_start(out=bias_rows[:], in_=fc1_base_b.partition_broadcast(P))
 
-        silu_grouped = keep.tile([P, COLS, PACK], BF16, align_bytes=64)
+        w_codes = keep.tile([P, SPLINE_PASSES + 1, OUT_F], U32, align_bytes=64)
+        w_scales = keep.tile([P, SPLINE_PASSES + 1, OUT_F], U8, align_bytes=64)
+        silu_grouped = [keep.tile([P, ROUND_COLS, PACK], BF16, name="silu_grouped%d" % r, align_bytes=64) for r in range(ROUNDS)]
         silu_codes = keep.tile([P, COLS], U32, align_bytes=64)
         silu_scales = keep.tile([P, COLS], U8, align_bytes=64)
-        for b in range(BATCH):
+        transposed, w_grouped, shifted, arg, grouped, operand, acc = {}, {}, {}, {}, {}, {}, {}
+
+        def silu_activation(r):
             nc.scalar.activation(
-                out=silu_grouped[:, b * CHANNELS : (b + 1) * CHANNELS, :].rearrange("p (c i) t -> p c t i", i=RUN),
-                in_=x_four[b][:].rearrange("p t (c i) -> p c t i", i=RUN),
+                out=silu_grouped[r][:].rearrange("p (c i) t -> p c t i", i=RUN),
+                in_=x_four[r][:].rearrange("p t (c i) -> p c t i", i=RUN),
                 func=ACT.Silu,
             )
-        for r in range(ROUNDS):
+
+        def silu_quantise(r):
             cols = slice(r * ROUND_COLS, (r + 1) * ROUND_COLS)
             nc.vector.quantize_mx(
                 out=silu_codes[:, cols].bitcast(FP8X4),
                 scales=silu_scales[:, cols],
-                in_=silu_grouped[:, cols, :].rearrange("p c t -> p (c t)"),
+                in_=silu_grouped[r][:].rearrange("p c t -> p (c t)"),
             )
 
-        w_codes = keep.tile([P, SPLINE_PASSES + 1, OUT_F], U32, align_bytes=64)
-        w_scales = keep.tile([P, SPLINE_PASSES + 1, OUT_F], U8, align_bytes=64)
-
-        def prepare_weights(w):
+        def weights_transpose(w):
             words = w_raw[w][:].bitcast(F32)
-            w_grouped = w_grouped_pool.tile([P, OUT_F * PACK], BF16, align_bytes=64)
-            grouped_words = w_grouped[:].bitcast(F32)
             for half in range(2):
-                wt = psum_wt.tile([P, 2, 2 * P], F32)
+                wt = psum_wt.tile([P, 2, 2 * P], F32, name="wt")
                 for o_local in range(2):
                     first = (2 * half + o_local) * (K_PASS // 2)
                     for u in range(2):
@@ -123,91 +157,144 @@ def tile_kan1_pa_kernel(tc, x, fc1_spline_w, fc1_base_w, fc1_base_b, out):
                             words[:, first + u : first + K_PASS // 2 : 2],
                             ident[:],
                         )
+                transposed[(w, half)] = wt
+
+        def weights_copy(w):
+            w_grouped[w] = w_grouped_pool.tile([P, OUT_F * PACK], BF16, name="w_grouped", align_bytes=64)
+            grouped_words = w_grouped[w][:].bitcast(F32)
+            for half in range(2):
                 nc.scalar.copy(
                     out=grouped_words[:, half * 4 * P : (half + 1) * 4 * P].rearrange("p (o u) -> p o u", u=2),
-                    in_=wt[:].rearrange("p u o -> p o u"),
+                    in_=transposed[(w, half)][:].rearrange("p u o -> p o u"),
                 )
-            nc.vector.quantize_mx(out=w_codes[:, w, :].bitcast(FP8X4), scales=w_scales[:, w, :], in_=w_grouped[:])
 
-        def basis_operand(r, g):
-            cols = slice(r * ROUND_COLS, (r + 1) * ROUND_COLS)
-            x_rows = x_twice[g // 2][:, g % 2, cols]
-            arg = arg_pool.tile([P, PACK, ROUND_COLS], F32)
-            if g % 4 == 3:
+        def weights_quantise(w):
+            nc.vector.quantize_mx(out=w_codes[:, w, :].bitcast(FP8X4), scales=w_scales[:, w, :], in_=w_grouped[w][:])
+
+        def x_rows(s):
+            r, g = divmod(s, SPLINE_PASSES)
+            return x_twice[r][g // PASSES_PER_LOAD][:, g % PASSES_PER_LOAD, :]
+
+        def shift(s):
+            r, g = divmod(s, SPLINE_PASSES)
+            if squared_on_scalar(r, g):
+                return
+            shifted[s] = shifted_pool.tile([P, 2, ROUND_COLS], F32, name="shifted")
+            for u in range(2):
+                nc.vector.tensor_scalar(
+                    out=shifted[s][:, u, :],
+                    in0=x_rows(s),
+                    scalar1=3.5,
+                    scalar2=pair_mid[:, u : u + 1],
+                    op0=ALU.mult,
+                    op1=ALU.subtract,
+                )
+
+        def square(s):
+            r, g = divmod(s, SPLINE_PASSES)
+            arg[s] = arg_pool.tile([P, PACK, ROUND_COLS], F32, name="arg")
+            if squared_on_scalar(r, g):
                 for t in range(PACK):
                     nc.scalar.activation(
-                        out=arg[:, t, :], in_=x_rows, func=ACT.Square, bias=neg_centre[:, t : t + 1], scale=3.5
+                        out=arg[s][:, t, :], in_=x_rows(s), func=ACT.Square, bias=neg_centre[:, t : t + 1], scale=3.5
                     )
-                exp_bias = 0.0
             else:
-                shifted = shifted_pool.tile([P, 2, ROUND_COLS], F32)
-                for u in range(2):
-                    nc.vector.tensor_scalar(
-                        out=shifted[:, u, :],
-                        in0=x_rows,
-                        scalar1=3.5,
-                        scalar2=pair_mid[:, u : u + 1],
-                        op0=ALU.mult,
-                        op1=ALU.subtract,
-                    )
-                arg_by_e = arg[:].rearrange("p (u e) c -> p e u c", e=2)
+                arg_by_e = arg[s][:].rearrange("p (u e) c -> p e u c", e=2)
                 for e in range(2):
                     nc.vector.scalar_tensor_tensor(
                         out=arg_by_e[:, e, :, :],
-                        in0=shifted[:],
+                        in0=shifted[s][:],
                         scalar=2.0 * e - 1.0,
-                        in1=shifted[:],
+                        in1=shifted[s][:],
                         op0=ALU.subtract,
                         op1=ALU.mult,
                     )
-                exp_bias = -0.25
-            grouped = grouped_pool.tile([P, ROUND_COLS, PACK], BF16, align_bytes=64)
+
+        def exponential(s):
+            r, g = divmod(s, SPLINE_PASSES)
+            grouped[s] = grouped_pool.tile([P, ROUND_COLS, PACK], BF16, name="grouped", align_bytes=64)
             nc.scalar.activation(
-                out=grouped[:].rearrange("p (c i) t -> p c t i", i=RUN),
-                in_=arg[:].rearrange("p t (c i) -> p c t i", i=RUN),
+                out=grouped[s][:].rearrange("p (c i) t -> p c t i", i=RUN),
+                in_=arg[s][:].rearrange("p t (c i) -> p c t i", i=RUN),
                 func=ACT.Exp,
-                bias=exp_bias,
+                bias=0.0 if squared_on_scalar(r, g) else -0.25,
                 scale=-1.0,
             )
-            codes = operand_pool.tile([P, ROUND_COLS], U32, align_bytes=64)
-            scales = operand_pool.tile([P, ROUND_COLS], U8, align_bytes=64)
-            nc.vector.quantize_mx(
-                out=codes[:].bitcast(FP8X4), scales=scales[:], in_=grouped[:].rearrange("p c t -> p (c t)")
-            )
-            return codes, scales
 
-        for r in range(ROUNDS):
-            acc = [psum_acc.tile([P, OUT_F], F32, name="acc", tag="acc") for j in range(M_TILES)]
-            if r == 0:
-                prepare_weights(BASE)
-            for j in range(M_TILES):
-                m_cols = slice(r * ROUND_COLS + j * P, r * ROUND_COLS + (j + 1) * P)
-                nc.tensor.matmul_mx(
-                    out=acc[j][:],
-                    lhsT=silu_codes[:, m_cols].bitcast(FP8X4),
-                    lhsT_scale=silu_scales[:, m_cols],
-                    rhs=w_codes[:, BASE, :].bitcast(FP8X4),
-                    rhs_scale=w_scales[:, BASE, :],
-                    start=True,
-                    stop=False,
-                )
-            for g in range(SPLINE_PASSES):
-                if r == 0:
-                    prepare_weights(g)
-                codes, scales = basis_operand(r, g)
+        def quantise(s):
+            codes = operand_pool.tile([P, ROUND_COLS], U32, name="codes", align_bytes=64)
+            scales = operand_pool.tile([P, ROUND_COLS], U8, name="scales", align_bytes=64)
+            nc.vector.quantize_mx(
+                out=codes[:].bitcast(FP8X4), scales=scales[:], in_=grouped[s][:].rearrange("p c t -> p (c t)")
+            )
+            operand[s] = (codes, scales)
+
+        def multiply(s):
+            r, g = divmod(s, SPLINE_PASSES)
+            if g == 0:
                 for j in range(M_TILES):
-                    m_cols = slice(j * P, (j + 1) * P)
+                    acc[j] = psum_acc.tile([P, OUT_F], F32, name="acc")
+                    m_cols = slice(r * ROUND_COLS + j * P, r * ROUND_COLS + (j + 1) * P)
                     nc.tensor.matmul_mx(
                         out=acc[j][:],
-                        lhsT=codes[:, m_cols].bitcast(FP8X4),
-                        lhsT_scale=scales[:, m_cols],
-                        rhs=w_codes[:, g, :].bitcast(FP8X4),
-                        rhs_scale=w_scales[:, g, :],
-                        start=False,
-                        stop=(g == SPLINE_PASSES - 1),
+                        lhsT=silu_codes[:, m_cols].bitcast(FP8X4),
+                        lhsT_scale=silu_scales[:, m_cols],
+                        rhs=w_codes[:, BASE, :].bitcast(FP8X4),
+                        rhs_scale=w_scales[:, BASE, :],
+                        start=True,
+                        stop=False,
                     )
+            codes, scales = operand[s]
             for j in range(M_TILES):
-                result = result_pool.tile([P, OUT_F], F32)
+                m_cols = slice(j * P, (j + 1) * P)
+                nc.tensor.matmul_mx(
+                    out=acc[j][:],
+                    lhsT=codes[:, m_cols].bitcast(FP8X4),
+                    lhsT_scale=scales[:, m_cols],
+                    rhs=w_codes[:, g, :].bitcast(FP8X4),
+                    rhs_scale=w_scales[:, g, :],
+                    start=False,
+                    stop=(g == SPLINE_PASSES - 1),
+                )
+
+        def finish_round(r):
+            for j in range(M_TILES):
+                result = result_pool.tile([P, OUT_F], F32, name="result")
                 nc.vector.tensor_tensor(out=result[:], in0=acc[j][:], in1=bias_rows[:], op=ALU.add)
                 first_row = r * ROUND_COLS + j * P
                 nc.sync.dma_start(out=out_rows[first_row : first_row + P, :], in_=result[:])
+
+        shift(0)
+        shift(1)
+        square(0)
+        weights_transpose(BASE)
+        weights_transpose(0)
+        silu_activation(0)
+        weights_copy(BASE)
+        silu_activation(1)
+        silu_activation(2)
+        for i in range(1 - LEAD, STEPS + 1):
+            ahead = i + LEAD
+            if ahead + 1 < STEPS:
+                shift(ahead + 1)
+            if ahead < STEPS:
+                square(ahead)
+            if i == 0:
+                for r in range(ROUNDS):
+                    silu_quantise(r)
+                weights_quantise(BASE)
+            if 0 <= i < SPLINE_PASSES:
+                if i + 1 < SPLINE_PASSES:
+                    weights_transpose(i + 1)
+                weights_copy(i)
+            if 0 <= i < STEPS:
+                exponential(i)
+            done = i - 1
+            if done >= 0:
+                quantise(done)
+                if done < SPLINE_PASSES:
+                    weights_quantise(done)
+                if done >= SPLINE_PASSES and done % SPLINE_PASSES == 0:
+                    finish_round(done // SPLINE_PASSES - 1)
+                multiply(done)
+        finish_round(ROUNDS - 1)

@@ -50,230 +50,236 @@ def tile_kan1_pa_kernel(tc, x, fc1_spline_w, fc1_base_w, fc1_base_b, out):
         psum_acc = ctx.enter_context(tc.psum_pool(name="psum_acc", bufs=M_TILES))
         psum_wt = ctx.enter_context(tc.psum_pool(name="psum_wt", bufs=4))
 
-        ident = keep.tile([P, P], F32)
-        make_identity(nc, ident[:])
-        odd = keep.tile([P, 1], F32)
-        nc.vector.reduce_sum(out=odd[:], in_=ident[:, 1:P:2], axis=mybir.AxisListType.X)
-        pair_mid = keep.tile([P, 2], F32)
-        for u in range(2):
-            nc.vector.tensor_scalar(
-                out=pair_mid[:, u : u + 1], in0=odd[:], scalar1=4.0, scalar2=2.0 * u - 3.0, op0=ALU.mult, op1=ALU.add
-            )
-        neg_centre = keep.tile([P, PACK], F32)
-        for t in range(PACK):
-            nc.vector.tensor_scalar(
-                out=neg_centre[:, t : t + 1], in0=odd[:], scalar1=-4.0, scalar2=3.5 - t, op0=ALU.mult, op1=ALU.add
-            )
-        bias_rows = keep.tile([P, OUT_F], BF16)
-
-        loads_per_round = SPLINE_PASSES // PASSES_PER_LOAD
-        x_twice = [
-            [keep.tile([P, PASSES_PER_LOAD, ROUND_COLS], BF16, name="x_twice%d_%d" % (r, h)) for h in range(loads_per_round)]
-            for r in range(ROUNDS)
-        ]
-        x_four = [keep.tile([P, PACK, ROUND_COLS], BF16, name="x_four%d" % r) for r in range(ROUNDS)]
-        w_raw = [keep.tile([P, PACK * K_PASS], BF16, name="w_raw%d" % w) for w in range(SPLINE_PASSES + 1)]
-
-        def column_pieces(r):
-            pieces = []
-            for b in range(BATCH):
-                lo = max(r * ROUND_COLS, b * CHANNELS)
-                hi = min((r + 1) * ROUND_COLS, (b + 1) * CHANNELS)
-                if lo < hi:
-                    pieces.append((b, lo - b * CHANNELS, hi - b * CHANNELS, lo - r * ROUND_COLS))
-            return pieces
-
-        def load_x_twice(r, h):
-            patches = slice(PASSES_PER_LOAD * PATCHES_PER_PASS * h, PASSES_PER_LOAD * PATCHES_PER_PASS * (h + 1))
-            for b, c_lo, c_hi, col in column_pieces(r):
-                for parity in range(2):
-                    nc.sync.dma_start(
-                        out=x_twice[r][h][parity:P:2, :, col : col + c_hi - c_lo],
-                        in_=x[b, patches, c_lo:c_hi].rearrange("(g a) c -> a g c", a=PATCHES_PER_PASS),
-                    )
-
-        def load_x_four(r):
-            for b, c_lo, c_hi, col in column_pieces(r):
-                nc.sync.dma_start(
-                    out=x_four[r][:, :, col : col + c_hi - c_lo],
-                    in_=x[b, :, c_lo:c_hi].rearrange("(q t) c -> q t c", t=PACK),
-                )
-
-        def load_weights(w):
-            source = fc1_base_w if w == BASE else fc1_spline_w[:, w * K_PASS : (w + 1) * K_PASS]
-            nc.sync.dma_start(
-                out=w_raw[w][:].rearrange("p (ot k) -> p ot k", k=K_PASS),
-                in_=source.rearrange("(ot p) k -> p ot k", p=P),
-            )
-
-        load_x_twice(0, 0)
-        load_x_four(0)
-        load_x_twice(0, 1)
-        load_weights(BASE)
-        load_x_four(1)
-        load_x_four(2)
-        load_x_twice(0, 2)
-        load_weights(0)
-        load_weights(1)
-        load_x_twice(0, 3)
-        for w in range(2, SPLINE_PASSES):
-            load_weights(w)
-        for r in range(1, ROUNDS):
-            for h in range(loads_per_round):
-                load_x_twice(r, h)
-        nc.sync.dma_start(out=bias_rows[:], in_=fc1_base_b.partition_broadcast(P))
-
-        w_codes = keep.tile([P, SPLINE_PASSES + 1, OUT_F], U32, align_bytes=64)
-        w_scales = keep.tile([P, SPLINE_PASSES + 1, OUT_F], U8, align_bytes=64)
-        silu_grouped = [keep.tile([P, ROUND_COLS, PACK], BF16, name="silu_grouped%d" % r, align_bytes=64) for r in range(ROUNDS)]
-        silu_codes = keep.tile([P, COLS], U32, align_bytes=64)
-        silu_scales = keep.tile([P, COLS], U8, align_bytes=64)
-        transposed, w_grouped, shifted, arg, grouped, operand, acc = {}, {}, {}, {}, {}, {}, {}
-
-        def silu_activation(r):
-            nc.scalar.activation(
-                out=silu_grouped[r][:].rearrange("p (c i) t -> p c t i", i=RUN),
-                in_=x_four[r][:].rearrange("p t (c i) -> p c t i", i=RUN),
-                func=ACT.Silu,
-            )
-
-        def silu_quantise(r):
-            cols = slice(r * ROUND_COLS, (r + 1) * ROUND_COLS)
-            nc.vector.quantize_mx(
-                out=silu_codes[:, cols].bitcast(FP8X4),
-                scales=silu_scales[:, cols],
-                in_=silu_grouped[r][:].rearrange("p c t -> p (c t)"),
-            )
-
-        def weights_transpose(w):
-            words = w_raw[w][:].bitcast(F32)
-            for half in range(2):
-                wt = psum_wt.tile([P, 2, 2 * P], F32, name="wt")
-                for o_local in range(2):
-                    first = (2 * half + o_local) * (K_PASS // 2)
-                    for u in range(2):
-                        nc.tensor.transpose(
-                            wt[:, u, o_local * P : (o_local + 1) * P],
-                            words[:, first + u : first + K_PASS // 2 : 2],
-                            ident[:],
-                        )
-                transposed[(w, half)] = wt
-
-        def weights_copy(w):
-            w_grouped[w] = w_grouped_pool.tile([P, OUT_F * PACK], BF16, name="w_grouped", align_bytes=64)
-            grouped_words = w_grouped[w][:].bitcast(F32)
-            for half in range(2):
-                nc.scalar.copy(
-                    out=grouped_words[:, half * 4 * P : (half + 1) * 4 * P].rearrange("p (o u) -> p o u", u=2),
-                    in_=transposed[(w, half)][:].rearrange("p u o -> p o u"),
-                )
-
-        def weights_quantise(w):
-            nc.vector.quantize_mx(out=w_codes[:, w, :].bitcast(FP8X4), scales=w_scales[:, w, :], in_=w_grouped[w][:])
-
-        def x_rows(s):
-            r, g = divmod(s, SPLINE_PASSES)
-            return x_twice[r][g // PASSES_PER_LOAD][:, g % PASSES_PER_LOAD, :]
-
-        def shift(s):
-            r, g = divmod(s, SPLINE_PASSES)
-            if squared_on_scalar(r, g):
-                return
-            shifted[s] = shifted_pool.tile([P, 2, ROUND_COLS], F32, name="shifted")
+        with tc.manual_schedule():
+            ident = keep.tile([P, P], F32)
+            make_identity(nc, ident[:])
+            odd = keep.tile([P, 1], F32)
+            nc.vector.reduce_sum(out=odd[:], in_=ident[:, 1:P:2], axis=mybir.AxisListType.X)
+            pair_mid = keep.tile([P, 2], F32)
             for u in range(2):
                 nc.vector.tensor_scalar(
-                    out=shifted[s][:, u, :],
-                    in0=x_rows(s),
-                    scalar1=3.5,
-                    scalar2=pair_mid[:, u : u + 1],
-                    op0=ALU.mult,
-                    op1=ALU.subtract,
+                    out=pair_mid[:, u : u + 1], in0=odd[:], scalar1=4.0, scalar2=2.0 * u - 3.0, op0=ALU.mult, op1=ALU.add
+                )
+            neg_centre = keep.tile([P, PACK], F32)
+            for t in range(PACK):
+                nc.vector.tensor_scalar(
+                    out=neg_centre[:, t : t + 1], in0=odd[:], scalar1=-4.0, scalar2=3.5 - t, op0=ALU.mult, op1=ALU.add
+                )
+            bias_rows = keep.tile([P, OUT_F], BF16)
+            table_warmer = keep.tile([P, 1], F32)
+            nc.scalar.activation(out=table_warmer[:], in_=odd[:], func=ACT.Silu)
+
+            loads_per_round = SPLINE_PASSES // PASSES_PER_LOAD
+            x_twice = [
+                [keep.tile([P, PASSES_PER_LOAD, ROUND_COLS], BF16, name="x_twice%d_%d" % (r, h)) for h in range(loads_per_round)]
+                for r in range(ROUNDS)
+            ]
+            x_four = [keep.tile([P, PACK, ROUND_COLS], BF16, name="x_four%d" % r) for r in range(ROUNDS)]
+            w_raw = [keep.tile([P, PACK * K_PASS], BF16, name="w_raw%d" % w) for w in range(SPLINE_PASSES + 1)]
+
+            def column_pieces(r):
+                pieces = []
+                for b in range(BATCH):
+                    lo = max(r * ROUND_COLS, b * CHANNELS)
+                    hi = min((r + 1) * ROUND_COLS, (b + 1) * CHANNELS)
+                    if lo < hi:
+                        pieces.append((b, lo - b * CHANNELS, hi - b * CHANNELS, lo - r * ROUND_COLS))
+                return pieces
+
+            def load_x_twice(r, h):
+                patches = slice(PASSES_PER_LOAD * PATCHES_PER_PASS * h, PASSES_PER_LOAD * PATCHES_PER_PASS * (h + 1))
+                for b, c_lo, c_hi, col in column_pieces(r):
+                    for parity in range(2):
+                        nc.sync.dma_start(
+                            out=x_twice[r][h][parity:P:2, :, col : col + c_hi - c_lo],
+                            in_=x[b, patches, c_lo:c_hi].rearrange("(g a) c -> a g c", a=PATCHES_PER_PASS),
+                        )
+
+            def load_x_four(r):
+                for b, c_lo, c_hi, col in column_pieces(r):
+                    nc.sync.dma_start(
+                        out=x_four[r][:, :, col : col + c_hi - c_lo],
+                        in_=x[b, :, c_lo:c_hi].rearrange("(q t) c -> q t c", t=PACK),
+                    )
+
+            def load_weights(w):
+                source = fc1_base_w if w == BASE else fc1_spline_w[:, w * K_PASS : (w + 1) * K_PASS]
+                nc.sync.dma_start(
+                    out=w_raw[w][:].rearrange("p (ot k) -> p ot k", k=K_PASS),
+                    in_=source.rearrange("(ot p) k -> p ot k", p=P),
                 )
 
-        def square(s):
-            r, g = divmod(s, SPLINE_PASSES)
-            arg[s] = arg_pool.tile([P, PACK, ROUND_COLS], F32, name="arg")
-            if squared_on_scalar(r, g):
-                for t in range(PACK):
-                    nc.scalar.activation(
-                        out=arg[s][:, t, :], in_=x_rows(s), func=ACT.Square, bias=neg_centre[:, t : t + 1], scale=3.5
+            load_x_twice(0, 0)
+            load_x_four(0)
+            load_x_twice(0, 1)
+            load_weights(BASE)
+            load_x_four(1)
+            load_x_four(2)
+            load_x_twice(0, 2)
+            load_weights(0)
+            load_weights(1)
+            load_x_twice(0, 3)
+            for w in range(2, SPLINE_PASSES):
+                load_weights(w)
+            for r in range(1, ROUNDS):
+                for h in range(loads_per_round):
+                    load_x_twice(r, h)
+            nc.sync.dma_start(out=bias_rows[:], in_=fc1_base_b.partition_broadcast(P))
+
+            w_codes = keep.tile([P, SPLINE_PASSES + 1, OUT_F], U32, align_bytes=64)
+            w_scales = keep.tile([P, SPLINE_PASSES + 1, OUT_F], U8, align_bytes=64)
+            silu_grouped = [keep.tile([P, ROUND_COLS, PACK], BF16, name="silu_grouped%d" % r, align_bytes=64) for r in range(ROUNDS)]
+            silu_codes = keep.tile([P, COLS], U32, align_bytes=64)
+            silu_scales = keep.tile([P, COLS], U8, align_bytes=64)
+            transposed, w_grouped, shifted, arg, grouped, operand, acc = {}, {}, {}, {}, {}, {}, {}
+
+            def silu_activation(r):
+                nc.scalar.activation(
+                    out=silu_grouped[r][:].rearrange("p (c i) t -> p c t i", i=RUN),
+                    in_=x_four[r][:].rearrange("p t (c i) -> p c t i", i=RUN),
+                    func=ACT.Silu,
+                )
+
+            def silu_quantise(r):
+                cols = slice(r * ROUND_COLS, (r + 1) * ROUND_COLS)
+                nc.vector.quantize_mx(
+                    out=silu_codes[:, cols].bitcast(FP8X4),
+                    scales=silu_scales[:, cols],
+                    in_=silu_grouped[r][:].rearrange("p c t -> p (c t)"),
+                )
+
+            def weights_transpose(w):
+                words = w_raw[w][:].bitcast(F32)
+                for half in range(2):
+                    wt = psum_wt.tile([P, 2, 2 * P], F32, name="wt")
+                    for o_local in range(2):
+                        first = (2 * half + o_local) * (K_PASS // 2)
+                        for u in range(2):
+                            nc.tensor.transpose(
+                                wt[:, u, o_local * P : (o_local + 1) * P],
+                                words[:, first + u : first + K_PASS // 2 : 2],
+                                ident[:],
+                            )
+                    transposed[(w, half)] = wt
+
+            def weights_copy(w):
+                w_grouped[w] = w_grouped_pool.tile([P, OUT_F * PACK], BF16, name="w_grouped", align_bytes=64)
+                grouped_words = w_grouped[w][:].bitcast(F32)
+                for half in range(2):
+                    nc.scalar.copy(
+                        out=grouped_words[:, half * 4 * P : (half + 1) * 4 * P].rearrange("p (o u) -> p o u", u=2),
+                        in_=transposed[(w, half)][:].rearrange("p u o -> p o u"),
                     )
-            else:
-                arg_by_e = arg[s][:].rearrange("p (u e) c -> p e u c", e=2)
-                for e in range(2):
-                    nc.vector.scalar_tensor_tensor(
-                        out=arg_by_e[:, e, :, :],
-                        in0=shifted[s][:],
-                        scalar=2.0 * e - 1.0,
-                        in1=shifted[s][:],
-                        op0=ALU.subtract,
-                        op1=ALU.mult,
+
+            def weights_quantise(w):
+                nc.vector.quantize_mx(out=w_codes[:, w, :].bitcast(FP8X4), scales=w_scales[:, w, :], in_=w_grouped[w][:])
+
+            def x_rows(s):
+                r, g = divmod(s, SPLINE_PASSES)
+                return x_twice[r][g // PASSES_PER_LOAD][:, g % PASSES_PER_LOAD, :]
+
+            def shift(s):
+                r, g = divmod(s, SPLINE_PASSES)
+                if squared_on_scalar(r, g):
+                    return
+                shifted[s] = shifted_pool.tile([P, 2, ROUND_COLS], F32, name="shifted")
+                for u in range(2):
+                    nc.vector.tensor_scalar(
+                        out=shifted[s][:, u, :],
+                        in0=x_rows(s),
+                        scalar1=3.5,
+                        scalar2=pair_mid[:, u : u + 1],
+                        op0=ALU.mult,
+                        op1=ALU.subtract,
                     )
 
-        def exponential(s):
-            r, g = divmod(s, SPLINE_PASSES)
-            grouped[s] = grouped_pool.tile([P, ROUND_COLS, PACK], BF16, name="grouped", align_bytes=64)
-            nc.scalar.activation(
-                out=grouped[s][:].rearrange("p (c i) t -> p c t i", i=RUN),
-                in_=arg[s][:].rearrange("p t (c i) -> p c t i", i=RUN),
-                func=ACT.Exp,
-                bias=0.0 if squared_on_scalar(r, g) else -0.25,
-                scale=-1.0,
-            )
+            def square(s):
+                r, g = divmod(s, SPLINE_PASSES)
+                arg[s] = arg_pool.tile([P, PACK, ROUND_COLS], F32, name="arg")
+                if squared_on_scalar(r, g):
+                    for t in range(PACK):
+                        nc.scalar.activation(
+                            out=arg[s][:, t, :], in_=x_rows(s), func=ACT.Square, bias=neg_centre[:, t : t + 1], scale=3.5
+                        )
+                else:
+                    arg_by_e = arg[s][:].rearrange("p (u e) c -> p e u c", e=2)
+                    for e in range(2):
+                        nc.vector.scalar_tensor_tensor(
+                            out=arg_by_e[:, e, :, :],
+                            in0=shifted[s][:],
+                            scalar=2.0 * e - 1.0,
+                            in1=shifted[s][:],
+                            op0=ALU.subtract,
+                            op1=ALU.mult,
+                        )
 
-        def quantise(s):
-            codes = operand_pool.tile([P, ROUND_COLS], U32, name="codes", align_bytes=64)
-            scales = operand_pool.tile([P, ROUND_COLS], U8, name="scales", align_bytes=64)
-            nc.vector.quantize_mx(
-                out=codes[:].bitcast(FP8X4), scales=scales[:], in_=grouped[s][:].rearrange("p c t -> p (c t)")
-            )
-            operand[s] = (codes, scales)
+            def exponential(s):
+                r, g = divmod(s, SPLINE_PASSES)
+                grouped[s] = grouped_pool.tile([P, ROUND_COLS, PACK], BF16, name="grouped", align_bytes=64)
+                nc.scalar.activation(
+                    out=grouped[s][:].rearrange("p (c i) t -> p c t i", i=RUN),
+                    in_=arg[s][:].rearrange("p t (c i) -> p c t i", i=RUN),
+                    func=ACT.Exp,
+                    bias=0.0 if squared_on_scalar(r, g) else -0.25,
+                    scale=-1.0,
+                )
 
-        def multiply(s):
-            r, g = divmod(s, SPLINE_PASSES)
-            if g == 0:
+            def quantise(s):
+                codes = operand_pool.tile([P, ROUND_COLS], U32, name="codes", align_bytes=64)
+                scales = operand_pool.tile([P, ROUND_COLS], U8, name="scales", align_bytes=64)
+                nc.vector.quantize_mx(
+                    out=codes[:].bitcast(FP8X4), scales=scales[:], in_=grouped[s][:].rearrange("p c t -> p (c t)")
+                )
+                operand[s] = (codes, scales)
+
+            def multiply(s):
+                r, g = divmod(s, SPLINE_PASSES)
+                if g == 0:
+                    for j in range(M_TILES):
+                        acc[j] = psum_acc.tile([P, OUT_F], F32, name="acc")
+                        m_cols = slice(r * ROUND_COLS + j * P, r * ROUND_COLS + (j + 1) * P)
+                        nc.tensor.matmul_mx(
+                            out=acc[j][:],
+                            lhsT=silu_codes[:, m_cols].bitcast(FP8X4),
+                            lhsT_scale=silu_scales[:, m_cols],
+                            rhs=w_codes[:, BASE, :].bitcast(FP8X4),
+                            rhs_scale=w_scales[:, BASE, :],
+                            start=True,
+                            stop=False,
+                        )
+                codes, scales = operand[s]
                 for j in range(M_TILES):
-                    acc[j] = psum_acc.tile([P, OUT_F], F32, name="acc")
-                    m_cols = slice(r * ROUND_COLS + j * P, r * ROUND_COLS + (j + 1) * P)
+                    m_cols = slice(j * P, (j + 1) * P)
                     nc.tensor.matmul_mx(
                         out=acc[j][:],
-                        lhsT=silu_codes[:, m_cols].bitcast(FP8X4),
-                        lhsT_scale=silu_scales[:, m_cols],
-                        rhs=w_codes[:, BASE, :].bitcast(FP8X4),
-                        rhs_scale=w_scales[:, BASE, :],
-                        start=True,
-                        stop=False,
+                        lhsT=codes[:, m_cols].bitcast(FP8X4),
+                        lhsT_scale=scales[:, m_cols],
+                        rhs=w_codes[:, g, :].bitcast(FP8X4),
+                        rhs_scale=w_scales[:, g, :],
+                        start=False,
+                        stop=(g == SPLINE_PASSES - 1),
                     )
-            codes, scales = operand[s]
-            for j in range(M_TILES):
-                m_cols = slice(j * P, (j + 1) * P)
-                nc.tensor.matmul_mx(
-                    out=acc[j][:],
-                    lhsT=codes[:, m_cols].bitcast(FP8X4),
-                    lhsT_scale=scales[:, m_cols],
-                    rhs=w_codes[:, g, :].bitcast(FP8X4),
-                    rhs_scale=w_scales[:, g, :],
-                    start=False,
-                    stop=(g == SPLINE_PASSES - 1),
-                )
 
-        def finish_round(r):
-            for j in range(M_TILES):
-                result = result_pool.tile([P, OUT_F], F32, name="result")
-                nc.vector.tensor_tensor(out=result[:], in0=acc[j][:], in1=bias_rows[:], op=ALU.add)
-                first_row = r * ROUND_COLS + j * P
-                nc.sync.dma_start(out=out_rows[first_row : first_row + P, :], in_=result[:])
+            def finish_round(r):
+                for j in range(M_TILES):
+                    result = result_pool.tile([P, OUT_F], F32, name="result")
+                    nc.vector.tensor_tensor(out=result[:], in0=acc[j][:], in1=bias_rows[:], op=ALU.add)
+                    first_row = r * ROUND_COLS + j * P
+                    nc.sync.dma_start(out=out_rows[first_row : first_row + P, :], in_=result[:])
 
-        shift(0)
-        shift(1)
-        square(0)
-        weights_transpose(BASE)
-        weights_transpose(0)
-        silu_activation(0)
-        weights_copy(BASE)
-        silu_activation(1)
-        silu_activation(2)
-        for i in range(1 - LEAD, STEPS + 1):
+            shift(0)
+            shift(1)
+            square(0)
+            weights_transpose(BASE)
+            weights_transpose(0)
+            silu_activation(0)
+            weights_copy(BASE)
+            silu_activation(1)
+            silu_activation(2)
+            for ahead in range(1, LEAD):
+                shift(ahead + 1)
+                square(ahead)
+        for i in range(0, STEPS + 1):
             ahead = i + LEAD
             if ahead + 1 < STEPS:
                 shift(ahead + 1)

@@ -39,7 +39,6 @@ def tile_kan1_pa_kernel(tc, x, fc1_spline_w, fc1_base_w, fc1_base_b, out):
     out_rows = out.flatten_outer_dims()
 
     with ExitStack() as ctx:
-        pass
         keep = ctx.enter_context(tc.tile_pool(name="keep", bufs=1))
         shifted_pool = ctx.enter_context(tc.tile_pool(name="shifted", bufs=3))
         arg_pool = ctx.enter_context(tc.tile_pool(name="arg", bufs=LEAD + 1))
@@ -224,6 +223,30 @@ def tile_kan1_pa_kernel(tc, x, fc1_spline_w, fc1_base_w, fc1_base_b, out):
                     scale=-1.0,
                 )
 
+            def exponential_tile(s, j):
+                r, g = divmod(s, SPLINE_PASSES)
+                if j == 0:
+                    grouped[s] = grouped_pool.tile([P, ROUND_COLS, PACK], BF16, name="grouped", align_bytes=64)
+                nc.scalar.activation(
+                    out=grouped[s][:, j * P : (j + 1) * P, :].rearrange("p (c i) t -> p c t i", i=RUN),
+                    in_=arg[s][:, :, j * P : (j + 1) * P].rearrange("p t (c i) -> p c t i", i=RUN),
+                    func=ACT.Exp,
+                    bias=0.0 if squared_on_scalar(r, g) else -0.25,
+                    scale=-1.0,
+                )
+
+            def quantise_tile(s, j):
+                if j == 0:
+                    codes = operand_pool.tile([P, ROUND_COLS], U32, name="codes", align_bytes=64)
+                    scales = operand_pool.tile([P, ROUND_COLS], U8, name="scales", align_bytes=64)
+                    operand[s] = (codes, scales)
+                codes, scales = operand[s]
+                nc.vector.quantize_mx(
+                    out=codes[:, j * P : (j + 1) * P].bitcast(FP8X4),
+                    scales=scales[:, j * P : (j + 1) * P],
+                    in_=grouped[s][:, j * P : (j + 1) * P, :].rearrange("p c t -> p (c t)"),
+                )
+
             def quantise(s):
                 codes = operand_pool.tile([P, ROUND_COLS], U32, name="codes", align_bytes=64)
                 scales = operand_pool.tile([P, ROUND_COLS], U8, name="scales", align_bytes=64)
@@ -232,7 +255,7 @@ def tile_kan1_pa_kernel(tc, x, fc1_spline_w, fc1_base_w, fc1_base_b, out):
                 )
                 operand[s] = (codes, scales)
 
-            def multiply(s):
+            def multiply(s, tiles=range(M_TILES)):
                 r, g = divmod(s, SPLINE_PASSES)
                 if g == 0:
                     for j in range(M_TILES):
@@ -248,7 +271,7 @@ def tile_kan1_pa_kernel(tc, x, fc1_spline_w, fc1_base_w, fc1_base_b, out):
                             stop=False,
                         )
                 codes, scales = operand[s]
-                for j in range(M_TILES):
+                for j in tiles:
                     m_cols = slice(j * P, (j + 1) * P)
                     nc.tensor.matmul_mx(
                         out=acc[j][:],
@@ -260,8 +283,8 @@ def tile_kan1_pa_kernel(tc, x, fc1_spline_w, fc1_base_w, fc1_base_b, out):
                         stop=(g == SPLINE_PASSES - 1),
                     )
 
-            def finish_round(r):
-                for j in range(M_TILES):
+            def finish_round(r, tiles=range(M_TILES)):
+                for j in tiles:
                     result = result_pool.tile([P, OUT_F], F32, name="result")
                     nc.vector.tensor_tensor(out=result[:], in0=acc[j][:], in1=bias_rows[:], op=ALU.add)
                     first_row = r * ROUND_COLS + j * P
@@ -279,7 +302,7 @@ def tile_kan1_pa_kernel(tc, x, fc1_spline_w, fc1_base_w, fc1_base_b, out):
             for ahead in range(1, LEAD):
                 shift(ahead + 1)
                 square(ahead)
-        for i in range(0, STEPS + 1):
+        for i in range(0, STEPS):
             ahead = i + LEAD
             if ahead + 1 < STEPS:
                 shift(ahead + 1)
@@ -293,7 +316,7 @@ def tile_kan1_pa_kernel(tc, x, fc1_spline_w, fc1_base_w, fc1_base_b, out):
                 if i + 1 < SPLINE_PASSES:
                     weights_transpose(i + 1)
                 weights_copy(i)
-            if 0 <= i < STEPS:
+            if i < STEPS - 1:
                 exponential(i)
             done = i - 1
             if done >= 0:
@@ -303,4 +326,12 @@ def tile_kan1_pa_kernel(tc, x, fc1_spline_w, fc1_base_w, fc1_base_b, out):
                 if done >= SPLINE_PASSES and done % SPLINE_PASSES == 0:
                     finish_round(done // SPLINE_PASSES - 1)
                 multiply(done)
-        finish_round(ROUNDS - 1)
+        last = STEPS - 1
+        for j in range(M_TILES):
+            exponential_tile(last, j)
+        for j in range(M_TILES):
+            quantise_tile(last, j)
+            multiply(last, (j,))
+            if j > 0:
+                finish_round(ROUNDS - 1, (j - 1,))
+        finish_round(ROUNDS - 1, (M_TILES - 1,))

@@ -30,8 +30,14 @@ LEAD = 4
 FLOPS = 2 * COLS * OUT_F * (PATCHES * CENTRES + PATCHES)
 
 
+EXPANDED = 7
+CHUNK = P // CENTRES
+ORDERS = ((0, 1, 2, 3, 4, 5, 6, 7), (0, 1, 2, 7, 3, 4, 5, 6), (0, 1, 2, 7, 3, 4, 5, 6))
+EXPAND_LEAD = (2, 4, 4)
+
+
 def squared_on_scalar(r, g):
-    return (r == 0 and g == 0) or (r > 0 and g % 3 == 2)
+    return (r == 0 and g == 0) or (r > 0 and g == 4)
 
 
 def tile_kan1_pa_kernel(tc, x, fc1_spline_w, fc1_base_w, fc1_base_b, out):
@@ -40,8 +46,9 @@ def tile_kan1_pa_kernel(tc, x, fc1_spline_w, fc1_base_w, fc1_base_b, out):
 
     with ExitStack() as ctx:
         keep = ctx.enter_context(tc.tile_pool(name="keep", bufs=1))
-        shifted_pool = ctx.enter_context(tc.tile_pool(name="shifted", bufs=3))
+        shifted_pool = ctx.enter_context(tc.tile_pool(name="shifted", bufs=2))
         arg_pool = ctx.enter_context(tc.tile_pool(name="arg", bufs=LEAD + 1))
+        product_pool = ctx.enter_context(tc.tile_pool(name="product", bufs=2))
         grouped_pool = ctx.enter_context(tc.tile_pool(name="grouped", bufs=4))
         operand_pool = ctx.enter_context(tc.tile_pool(name="operand", bufs=4))
         w_grouped_pool = ctx.enter_context(tc.tile_pool(name="w_grouped", bufs=4))
@@ -64,6 +71,65 @@ def tile_kan1_pa_kernel(tc, x, fc1_spline_w, fc1_base_w, fc1_base_b, out):
                 nc.vector.tensor_scalar(
                     out=neg_centre[:, t : t + 1], in0=odd[:], scalar1=-4.0, scalar2=3.5 - t, op0=ALU.mult, op1=ALU.add
                 )
+            ident_bf16 = keep.tile([P, P], BF16)
+            make_identity(nc, ident_bf16[:])
+            centre_row = keep.tile([P, CENTRES], F32)
+            for i in range(CENTRES):
+                nc.gpsimd.memset(centre_row[:, i : i + 1], i - 3.5)
+            second = keep.tile([P, 1], F32)
+            nc.vector.tensor_reduce(
+                out=second[:],
+                in_=ident[:].rearrange("p (j f rr) -> p j f rr", j=M_TILES, f=2)[:, :, 1, :],
+                axis=mybir.AxisListType.XY,
+                op=ALU.add,
+            )
+            row_shift = keep.tile([P, 1], F32)
+            nc.vector.tensor_scalar(out=row_shift[:], in0=second[:], scalar1=2.0, scalar2=None, op0=ALU.mult)
+            slope = keep.tile([P, 1], F32)
+            nc.vector.tensor_scalar(out=slope[:], in0=second[:], scalar1=-7.0, scalar2=3.5, op0=ALU.mult, op1=ALU.add)
+            level = keep.tile([P, 1], F32)
+            nc.vector.tensor_scalar(out=level[:], in0=second[:], scalar1=-12.25, scalar2=12.25, op0=ALU.mult, op1=ALU.add)
+            same_row = keep.tile([P, CHUNK], F32)
+            nc.vector.reduce_sum(
+                out=same_row[:], in_=ident[:].rearrange("p (g rr) -> p rr g", rr=CHUNK), axis=mybir.AxisListType.X
+            )
+            same_chunk = keep.tile([P, M_TILES], F32)
+            nc.vector.reduce_sum(
+                out=same_chunk[:], in_=ident[:].rearrange("p (j n) -> p j n", j=M_TILES), axis=mybir.AxisListType.X
+            )
+            coefficient = keep.tile([P, CENTRES], F32)
+            nc.vector.tensor_scalar(
+                out=coefficient[:], in0=centre_row[:], scalar1=slope[:], scalar2=level[:], op0=ALU.mult, op1=ALU.add
+            )
+            one_chunk = keep.tile([P, CHUNK, CENTRES], F32)
+            nc.vector.tensor_tensor(
+                out=one_chunk[:],
+                in0=same_row[:].unsqueeze(2).to_broadcast([P, CHUNK, CENTRES]),
+                in1=coefficient[:].unsqueeze(1).to_broadcast([P, CHUNK, CENTRES]),
+                op=ALU.mult,
+            )
+            by_column = keep.tile([P, P], F32)
+            nc.vector.tensor_tensor(
+                out=by_column[:].rearrange("p (a i) -> p a i", i=CENTRES),
+                in0=ident[:].rearrange("p (a i) -> p a i", i=CENTRES),
+                in1=centre_row[:].unsqueeze(1).to_broadcast([P, P // CENTRES, CENTRES]),
+                op=ALU.mult,
+            )
+            expand = keep.tile([P, M_TILES, P], F32)
+            for j in range(M_TILES):
+                nc.vector.tensor_scalar(
+                    out=expand[:, j, :],
+                    in0=one_chunk[:].rearrange("p a i -> p (a i)"),
+                    scalar1=same_chunk[:, j : j + 1],
+                    scalar2=None,
+                    op0=ALU.mult,
+                )
+            centre = keep.tile([P, 1], F32)
+            nc.vector.reduce_sum(out=centre[:], in_=by_column[:], axis=mybir.AxisListType.X)
+            neg_square = keep.tile([P, 1], F32)
+            nc.vector.scalar_tensor_tensor(
+                out=neg_square[:], in0=centre[:], scalar=-1.0, in1=centre[:], op0=ALU.mult, op1=ALU.mult
+            )
             bias_rows = keep.tile([P, OUT_F], BF16)
             table_warmer = keep.tile([P, 1], F32)
             nc.scalar.activation(out=table_warmer[:], in_=odd[:], func=ACT.Silu)
@@ -74,6 +140,7 @@ def tile_kan1_pa_kernel(tc, x, fc1_spline_w, fc1_base_w, fc1_base_b, out):
                 for r in range(ROUNDS)
             ]
             x_four = [keep.tile([P, PACK, ROUND_COLS], BF16, name="x_four%d" % r) for r in range(ROUNDS)]
+            x_chunks = [keep.tile([P, PACK, P], BF16, name="x_chunks%d" % r) for r in range(ROUNDS)]
             w_raw = [keep.tile([P, PACK * K_PASS], BF16, name="w_raw%d" % w) for w in range(SPLINE_PASSES + 1)]
 
             def column_pieces(r):
@@ -92,6 +159,16 @@ def tile_kan1_pa_kernel(tc, x, fc1_spline_w, fc1_base_w, fc1_base_b, out):
                         nc.sync.dma_start(
                             out=x_twice[r][h][parity:P:2, :, col : col + c_hi - c_lo],
                             in_=x[b, patches, c_lo:c_hi].rearrange("(g a) c -> a g c", a=PATCHES_PER_PASS),
+                        )
+
+            def load_x_chunks(r):
+                patches = slice(PATCHES_PER_PASS * EXPANDED, PATCHES_PER_PASS * (EXPANDED + 1))
+                for j in range(M_TILES):
+                    b, c_lo = divmod(r * ROUND_COLS + j * P, CHANNELS)
+                    for f in range(2):
+                        nc.sync.dma_start(
+                            out=x_chunks[r][32 * j + CHUNK * f : 32 * j + CHUNK * (f + 1), :, :],
+                            in_=x[b, patches, c_lo : c_lo + P].rearrange("(t rr) c -> rr t c", rr=CHUNK),
                         )
 
             def load_x_four(r):
@@ -120,7 +197,9 @@ def tile_kan1_pa_kernel(tc, x, fc1_spline_w, fc1_base_w, fc1_base_b, out):
             load_x_twice(0, 3)
             for w in range(2, SPLINE_PASSES):
                 load_weights(w)
+            load_x_chunks(0)
             for r in range(1, ROUNDS):
+                load_x_chunks(r)
                 for h in range(loads_per_round):
                     load_x_twice(r, h)
             nc.sync.dma_start(out=bias_rows[:], in_=fc1_base_b.partition_broadcast(P))
@@ -130,7 +209,7 @@ def tile_kan1_pa_kernel(tc, x, fc1_spline_w, fc1_base_w, fc1_base_b, out):
             silu_grouped = [keep.tile([P, ROUND_COLS, PACK], BF16, name="silu_grouped%d" % r, align_bytes=64) for r in range(ROUNDS)]
             silu_codes = keep.tile([P, COLS], U32, align_bytes=64)
             silu_scales = keep.tile([P, COLS], U8, align_bytes=64)
-            transposed, w_grouped, shifted, arg, grouped, operand, acc = {}, {}, {}, {}, {}, {}, {}
+            transposed, w_grouped, shifted, arg, grouped, operand, acc, product, exponents = [{} for n in range(9)]
 
             def silu_activation(r):
                 nc.scalar.activation(
@@ -150,42 +229,63 @@ def tile_kan1_pa_kernel(tc, x, fc1_spline_w, fc1_base_w, fc1_base_b, out):
             def weights_transpose(w):
                 words = w_raw[w][:].bitcast(F32)
                 for half in range(2):
-                    wt = psum_wt.tile([P, 2, 2 * P], F32, name="wt")
-                    for o_local in range(2):
-                        first = (2 * half + o_local) * (K_PASS // 2)
-                        for u in range(2):
-                            nc.tensor.transpose(
-                                wt[:, u, o_local * P : (o_local + 1) * P],
-                                words[:, first + u : first + K_PASS // 2 : 2],
-                                ident[:],
-                            )
+                    if w == EXPANDED:
+                        wt = psum_wt.tile([P, PACK, 2 * P], BF16, name="wt")
+                        for o_local in range(2):
+                            for t in range(PACK):
+                                first = (2 * half + o_local) * K_PASS + t * P
+                                nc.tensor.transpose(
+                                    wt[:, t, o_local * P : (o_local + 1) * P], w_raw[w][:, first : first + P], ident_bf16[:]
+                                )
+                    else:
+                        wt = psum_wt.tile([P, 2, 2 * P], F32, name="wt")
+                        for o_local in range(2):
+                            first = (2 * half + o_local) * (K_PASS // 2)
+                            for u in range(2):
+                                nc.tensor.transpose(
+                                    wt[:, u, o_local * P : (o_local + 1) * P],
+                                    words[:, first + u : first + K_PASS // 2 : 2],
+                                    ident[:],
+                                )
                     transposed[(w, half)] = wt
 
             def weights_copy(w):
                 w_grouped[w] = w_grouped_pool.tile([P, OUT_F * PACK], BF16, name="w_grouped", align_bytes=64)
-                grouped_words = w_grouped[w][:].bitcast(F32)
                 for half in range(2):
+                    if w == EXPANDED:
+                        target, step = w_grouped[w][:, half * 8 * P : (half + 1) * 8 * P], PACK
+                    else:
+                        target, step = w_grouped[w][:].bitcast(F32)[:, half * 4 * P : (half + 1) * 4 * P], 2
                     nc.scalar.copy(
-                        out=grouped_words[:, half * 4 * P : (half + 1) * 4 * P].rearrange("p (o u) -> p o u", u=2),
+                        out=target.rearrange("p (o u) -> p o u", u=step),
                         in_=transposed[(w, half)][:].rearrange("p u o -> p o u"),
                     )
 
             def weights_quantise(w):
                 nc.vector.quantize_mx(out=w_codes[:, w, :].bitcast(FP8X4), scales=w_scales[:, w, :], in_=w_grouped[w][:])
 
+            def place(s):
+                r, pos = divmod(s, SPLINE_PASSES)
+                return r, ORDERS[r][pos]
+
             def x_rows(s):
-                r, g = divmod(s, SPLINE_PASSES)
+                r, g = place(s)
                 return x_twice[r][g // PASSES_PER_LOAD][:, g % PASSES_PER_LOAD, :]
 
+            def on_vector(r, g):
+                return g != EXPANDED and not squared_on_scalar(r, g)
+
             def shift(s):
-                r, g = divmod(s, SPLINE_PASSES)
-                if squared_on_scalar(r, g):
+                r, g = place(s)
+                h = g // PASSES_PER_LOAD
+                if not on_vector(r, g) or (r, h) in shifted:
                     return
-                shifted[s] = shifted_pool.tile([P, 2, ROUND_COLS], F32, name="shifted")
+                used = [k for k in range(PASSES_PER_LOAD) if on_vector(r, h * PASSES_PER_LOAD + k)]
+                shifted[(r, h)] = shifted_pool.tile([P, 2, PASSES_PER_LOAD, ROUND_COLS], F32, name="shifted")
                 for u in range(2):
                     nc.vector.tensor_scalar(
-                        out=shifted[s][:, u, :],
-                        in0=x_rows(s),
+                        out=shifted[(r, h)][:, u, used[0] : used[-1] + 1, :],
+                        in0=x_twice[r][h][:, used[0] : used[-1] + 1, :],
                         scalar1=3.5,
                         scalar2=pair_mid[:, u : u + 1],
                         op0=ALU.mult,
@@ -193,7 +293,14 @@ def tile_kan1_pa_kernel(tc, x, fc1_spline_w, fc1_base_w, fc1_base_b, out):
                     )
 
             def square(s):
-                r, g = divmod(s, SPLINE_PASSES)
+                r, g = place(s)
+                if g == EXPANDED:
+                    product[s] = product_pool.tile([P, PACK * P], F32, name="product")
+                    rows = x_chunks[r][:].rearrange("p t c -> p (t c)")
+                    nc.vector.scalar_tensor_tensor(
+                        out=product[s][:], in0=rows, scalar=row_shift[:], in1=rows, op0=ALU.add, op1=ALU.mult
+                    )
+                    return
                 arg[s] = arg_pool.tile([P, PACK, ROUND_COLS], F32, name="arg")
                 if squared_on_scalar(r, g):
                     for t in range(PACK):
@@ -202,19 +309,35 @@ def tile_kan1_pa_kernel(tc, x, fc1_spline_w, fc1_base_w, fc1_base_b, out):
                         )
                 else:
                     arg_by_e = arg[s][:].rearrange("p (u e) c -> p e u c", e=2)
+                    factor = shifted[(r, g // PASSES_PER_LOAD)][:, :, g % PASSES_PER_LOAD, :]
                     for e in range(2):
                         nc.vector.scalar_tensor_tensor(
                             out=arg_by_e[:, e, :, :],
-                            in0=shifted[s][:],
+                            in0=factor,
                             scalar=2.0 * e - 1.0,
-                            in1=shifted[s][:],
+                            in1=factor,
                             op0=ALU.subtract,
                             op1=ALU.mult,
                         )
 
+            def expand_products(s):
+                for j in range(M_TILES):
+                    exponents[(s, j)] = psum_wt.tile([P, PACK * P], F32, name="wt")
+                    nc.tensor.matmul(exponents[(s, j)][:], lhsT=expand[:, j, :], rhs=product[s][:], start=True, stop=True)
+
             def exponential(s):
-                r, g = divmod(s, SPLINE_PASSES)
+                r, g = place(s)
                 grouped[s] = grouped_pool.tile([P, ROUND_COLS, PACK], BF16, name="grouped", align_bytes=64)
+                if g == EXPANDED:
+                    for j in range(M_TILES):
+                        nc.scalar.activation(
+                            out=grouped[s][:, j * P : (j + 1) * P, :].rearrange("p (c i) t -> p c t i", i=RUN),
+                            in_=exponents[(s, j)][:].rearrange("p (t c i) -> p c t i", t=PACK, i=RUN),
+                            func=ACT.Exp,
+                            bias=neg_square[:],
+                            scale=-1.0,
+                        )
+                    return
                 nc.scalar.activation(
                     out=grouped[s][:].rearrange("p (c i) t -> p c t i", i=RUN),
                     in_=arg[s][:].rearrange("p t (c i) -> p c t i", i=RUN),
@@ -224,7 +347,7 @@ def tile_kan1_pa_kernel(tc, x, fc1_spline_w, fc1_base_w, fc1_base_b, out):
                 )
 
             def exponential_tile(s, j):
-                r, g = divmod(s, SPLINE_PASSES)
+                r, g = place(s)
                 if j == 0:
                     grouped[s] = grouped_pool.tile([P, ROUND_COLS, PACK], BF16, name="grouped", align_bytes=64)
                 nc.scalar.activation(
@@ -256,8 +379,8 @@ def tile_kan1_pa_kernel(tc, x, fc1_spline_w, fc1_base_w, fc1_base_b, out):
                 operand[s] = (codes, scales)
 
             def multiply(s, tiles=range(M_TILES)):
-                r, g = divmod(s, SPLINE_PASSES)
-                if g == 0:
+                r, g = place(s)
+                if s % SPLINE_PASSES == 0:
                     for j in range(M_TILES):
                         acc[j] = psum_acc.tile([P, OUT_F], F32, name="acc")
                         m_cols = slice(r * ROUND_COLS + j * P, r * ROUND_COLS + (j + 1) * P)
@@ -280,7 +403,7 @@ def tile_kan1_pa_kernel(tc, x, fc1_spline_w, fc1_base_w, fc1_base_b, out):
                         rhs=w_codes[:, g, :].bitcast(FP8X4),
                         rhs_scale=w_scales[:, g, :],
                         start=False,
-                        stop=(g == SPLINE_PASSES - 1),
+                        stop=(s % SPLINE_PASSES == SPLINE_PASSES - 1),
                     )
 
             def finish_round(r, tiles=range(M_TILES)):
@@ -303,6 +426,14 @@ def tile_kan1_pa_kernel(tc, x, fc1_spline_w, fc1_base_w, fc1_base_b, out):
                 shift(ahead + 1)
                 square(ahead)
         for i in range(0, STEPS):
+            done = i - 1
+            if done >= 0:
+                quantise(done)
+                if done < SPLINE_PASSES:
+                    weights_quantise(done)
+                if done >= SPLINE_PASSES and done % SPLINE_PASSES == 0:
+                    finish_round(done // SPLINE_PASSES - 1)
+                multiply(done)
             ahead = i + LEAD
             if ahead + 1 < STEPS:
                 shift(ahead + 1)
@@ -316,16 +447,12 @@ def tile_kan1_pa_kernel(tc, x, fc1_spline_w, fc1_base_w, fc1_base_b, out):
                 if i + 1 < SPLINE_PASSES:
                     weights_transpose(i + 1)
                 weights_copy(i)
+            for s in range(i + 1, min(i + LEAD + 1, STEPS)):
+                r, g = place(s)
+                if g == EXPANDED and s == i + EXPAND_LEAD[r]:
+                    expand_products(s)
             if i < STEPS - 1:
                 exponential(i)
-            done = i - 1
-            if done >= 0:
-                quantise(done)
-                if done < SPLINE_PASSES:
-                    weights_quantise(done)
-                if done >= SPLINE_PASSES and done % SPLINE_PASSES == 0:
-                    finish_round(done // SPLINE_PASSES - 1)
-                multiply(done)
         last = STEPS - 1
         for j in range(M_TILES):
             exponential_tile(last, j)

from contextlib import ExitStack

import concourse.mybir as mybir
from concourse.masks import make_identity

F32 = mybir.dt.float32
BF16 = mybir.dt.bfloat16
U32 = mybir.dt.uint32
U8 = mybir.dt.uint8
FP8X4 = mybir.dt.float8_e4m3fn_x4
ACT = mybir.ActivationFunctionType
ALU = mybir.AluOpType

P = 128
PACK = 4
K_PASS = P * PACK
BATCH, PATCHES, CHANNELS, OUT_F, CENTRES = 2, 512, 768, 512, 8
COLS = BATCH * CHANNELS
ROUND_COLS = 512
ROUNDS = COLS // ROUND_COLS
M_TILES = ROUND_COLS // P
SPLINE_PASSES = PATCHES * CENTRES // K_PASS
STEPS = ROUNDS * SPLINE_PASSES
BASE = SPLINE_PASSES
PATCHES_PER_PASS = K_PASS // CENTRES
PASSES_PER_LOAD = 2
RUN = 4
LEAD = 4

FLOPS = 2 * COLS * OUT_F * (PATCHES * CENTRES + PATCHES)


EXPANDED = 7
CHUNK = P // CENTRES
ORDERS = ((0, 1, 2, 3, 4, 5, 6, 7), (0, 1, 2, 7, 3, 4, 5, 6), (0, 1, 2, 7, 3, 4, 5, 6))
EXPAND_LEAD = (2, 4, 4)


def squared_on_scalar(r, g):
    return (r == 0 and g == 0) or (r > 0 and g == 4)


def tile_kan1_pa_kernel(tc, x, fc1_spline_w, fc1_base_w, fc1_base_b, out):
    nc = tc.nc
    out_rows = out.flatten_outer_dims()

    with ExitStack() as ctx:
        keep = ctx.enter_context(tc.tile_pool(name="keep", bufs=1))
        shifted_pool = ctx.enter_context(tc.tile_pool(name="shifted", bufs=2))
        arg_pool = ctx.enter_context(tc.tile_pool(name="arg", bufs=LEAD + 1))
        product_pool = ctx.enter_context(tc.tile_pool(name="product", bufs=2))
        grouped_pool = ctx.enter_context(tc.tile_pool(name="grouped", bufs=4))
        operand_pool = ctx.enter_context(tc.tile_pool(name="operand", bufs=4))
        w_grouped_pool = ctx.enter_context(tc.tile_pool(name="w_grouped", bufs=4))
        result_pool = ctx.enter_context(tc.tile_pool(name="result", bufs=4))
        psum_acc = ctx.enter_context(tc.psum_pool(name="psum_acc", bufs=M_TILES))
        psum_wt = ctx.enter_context(tc.psum_pool(name="psum_wt", bufs=4))

        with tc.manual_schedule():
            ident = keep.tile([P, P], F32)
            make_identity(nc, ident[:])
            odd = keep.tile([P, 1], F32)
            nc.vector.reduce_sum(out=odd[:], in_=ident[:, 1:P:2], axis=mybir.AxisListType.X)
            pair_mid = keep.tile([P, 2], F32)
            for u in range(2):
                nc.vector.tensor_scalar(
                    out=pair_mid[:, u : u + 1], in0=odd[:], scalar1=4.0, scalar2=2.0 * u - 3.0, op0=ALU.mult, op1=ALU.add
                )
            neg_centre = keep.tile([P, PACK], F32)
            for t in range(PACK):
                nc.vector.tensor_scalar(
                    out=neg_centre[:, t : t + 1], in0=odd[:], scalar1=-4.0, scalar2=3.5 - t, op0=ALU.mult, op1=ALU.add
                )
            ident_bf16 = keep.tile([P, P], BF16)
            make_identity(nc, ident_bf16[:])
            centre_row = keep.tile([P, CENTRES], F32)
            for i in range(CENTRES):
                nc.gpsimd.memset(centre_row[:, i : i + 1], i - 3.5)
            second = keep.tile([P, 1], F32)
            nc.vector.tensor_reduce(
                out=second[:],
                in_=ident[:].rearrange("p (j f rr) -> p j f rr", j=M_TILES, f=2)[:, :, 1, :],
                axis=mybir.AxisListType.XY,
                op=ALU.add,
            )
            row_shift = keep.tile([P, 1], F32)
            nc.vector.tensor_scalar(out=row_shift[:], in0=second[:], scalar1=2.0, scalar2=None, op0=ALU.mult)
            slope = keep.tile([P, 1], F32)
            nc.vector.tensor_scalar(out=slope[:], in0=second[:], scalar1=-7.0, scalar2=3.5, op0=ALU.mult, op1=ALU.add)
            level = keep.tile([P, 1], F32)
            nc.vector.tensor_scalar(out=level[:], in0=second[:], scalar1=-12.25, scalar2=12.25, op0=ALU.mult, op1=ALU.add)
            same_row = keep.tile([P, CHUNK], F32)
            nc.vector.reduce_sum(
                out=same_row[:], in_=ident[:].rearrange("p (g rr) -> p rr g", rr=CHUNK), axis=mybir.AxisListType.X
            )
            same_chunk = keep.tile([P, M_TILES], F32)
            nc.vector.reduce_sum(
                out=same_chunk[:], in_=ident[:].rearrange("p (j n) -> p j n", j=M_TILES), axis=mybir.AxisListType.X
            )
            coefficient = keep.tile([P, CENTRES], F32)
            nc.vector.tensor_scalar(
                out=coefficient[:], in0=centre_row[:], scalar1=slope[:], scalar2=level[:], op0=ALU.mult, op1=ALU.add
            )
            one_chunk = keep.tile([P, CHUNK, CENTRES], F32)
            nc.vector.tensor_tensor(
                out=one_chunk[:],
                in0=same_row[:].unsqueeze(2).to_broadcast([P, CHUNK, CENTRES]),
                in1=coefficient[:].unsqueeze(1).to_broadcast([P, CHUNK, CENTRES]),
                op=ALU.mult,
            )
            by_column = keep.tile([P, P], F32)
            nc.vector.tensor_tensor(
                out=by_column[:].rearrange("p (a i) -> p a i", i=CENTRES),
                in0=ident[:].rearrange("p (a i) -> p a i", i=CENTRES),
                in1=centre_row[:].unsqueeze(1).to_broadcast([P, P // CENTRES, CENTRES]),
                op=ALU.mult,
            )
            expand = keep.tile([P, M_TILES, P], F32)
            for j in range(M_TILES):
                nc.vector.tensor_scalar(
                    out=expand[:, j, :],
                    in0=one_chunk[:].rearrange("p a i -> p (a i)"),
                    scalar1=same_chunk[:, j : j + 1],
                    scalar2=None,
                    op0=ALU.mult,
                )
            centre = keep.tile([P, 1], F32)
            nc.vector.reduce_sum(out=centre[:], in_=by_column[:], axis=mybir.AxisListType.X)
            neg_square = keep.tile([P, 1], F32)
            nc.vector.scalar_tensor_tensor(
                out=neg_square[:], in0=centre[:], scalar=-1.0, in1=centre[:], op0=ALU.mult, op1=ALU.mult
            )
            bias_rows = keep.tile([P, OUT_F], BF16)
            table_warmer = keep.tile([P, 1], F32)
            nc.scalar.activation(out=table_warmer[:], in_=odd[:], func=ACT.Silu)

            loads_per_round = SPLINE_PASSES // PASSES_PER_LOAD
            x_twice = [
                [keep.tile([P, PASSES_PER_LOAD, ROUND_COLS], BF16, name="x_twice%d_%d" % (r, h)) for h in range(loads_per_round)]
                for r in range(ROUNDS)
            ]
            x_four = [keep.tile([P, PACK, ROUND_COLS], BF16, name="x_four%d" % r) for r in range(ROUNDS)]
            x_chunks = [keep.tile([P, PACK, P], BF16, name="x_chunks%d" % r) for r in range(ROUNDS)]
            w_raw = [keep.tile([P, PACK * K_PASS], BF16, name="w_raw%d" % w) for w in range(SPLINE_PASSES + 1)]

            def column_pieces(r):
                pieces = []
                for b in range(BATCH):
                    lo = max(r * ROUND_COLS, b * CHANNELS)
                    hi = min((r + 1) * ROUND_COLS, (b + 1) * CHANNELS)
                    if lo < hi:
                        pieces.append((b, lo - b * CHANNELS, hi - b * CHANNELS, lo - r * ROUND_COLS))
                return pieces

            def load_x_twice(r, h):
                patches = slice(PASSES_PER_LOAD * PATCHES_PER_PASS * h, PASSES_PER_LOAD * PATCHES_PER_PASS * (h + 1))
                for b, c_lo, c_hi, col in column_pieces(r):
                    for parity in range(2):
                        nc.sync.dma_start(
                            out=x_twice[r][h][parity:P:2, :, col : col + c_hi - c_lo],
                            in_=x[b, patches, c_lo:c_hi].rearrange("(g a) c -> a g c", a=PATCHES_PER_PASS),
                        )

            def load_x_chunks(r):
                patches = slice(PATCHES_PER_PASS * EXPANDED, PATCHES_PER_PASS * (EXPANDED + 1))
                for j in range(M_TILES):
                    b, c_lo = divmod(r * ROUND_COLS + j * P, CHANNELS)
                    for f in range(2):
                        nc.sync.dma_start(
                            out=x_chunks[r][32 * j + CHUNK * f : 32 * j + CHUNK * (f + 1), :, :],
                            in_=x[b, patches, c_lo : c_lo + P].rearrange("(t rr) c -> rr t c", rr=CHUNK),
                        )

            def load_x_four(r):
                for b, c_lo, c_hi, col in column_pieces(r):
                    nc.sync.dma_start(
                        out=x_four[r][:, :, col : col + c_hi - c_lo],
                        in_=x[b, :, c_lo:c_hi].rearrange("(q t) c -> q t c", t=PACK),
                    )

            def load_weights(w):
                source = fc1_base_w if w == BASE else fc1_spline_w[:, w * K_PASS : (w + 1) * K_PASS]
                nc.sync.dma_start(
                    out=w_raw[w][:].rearrange("p (ot k) -> p ot k", k=K_PASS),
                    in_=source.rearrange("(ot p) k -> p ot k", p=P),
                )

            load_x_twice(0, 0)
            load_x_four(0)
            load_x_twice(0, 1)
            load_weights(BASE)
            load_x_four(1)
            load_x_four(2)
            load_x_twice(0, 2)
            load_weights(0)
            load_weights(1)
            load_x_twice(0, 3)
            for w in range(2, SPLINE_PASSES):
                load_weights(w)
            load_x_chunks(0)
            for r in range(1, ROUNDS):
                load_x_chunks(r)
                for h in range(loads_per_round):
                    load_x_twice(r, h)
            nc.sync.dma_start(out=bias_rows[:], in_=fc1_base_b.partition_broadcast(P))

            w_codes = keep.tile([P, SPLINE_PASSES + 1, OUT_F], U32, align_bytes=64)
            w_scales = keep.tile([P, SPLINE_PASSES + 1, OUT_F], U8, align_bytes=64)
            silu_grouped = [keep.tile([P, ROUND_COLS, PACK], BF16, name="silu_grouped%d" % r, align_bytes=64) for r in range(ROUNDS)]
            silu_codes = keep.tile([P, COLS], U32, align_bytes=64)
            silu_scales = keep.tile([P, COLS], U8, align_bytes=64)
            transposed, w_grouped, shifted, arg, grouped, operand, acc, product, exponents = [{} for n in range(9)]

            def silu_activation(r):
                nc.scalar.activation(
                    out=silu_grouped[r][:].rearrange("p (c i) t -> p c t i", i=RUN),
                    in_=x_four[r][:].rearrange("p t (c i) -> p c t i", i=RUN),
                    func=ACT.Silu,
                )

            def silu_quantise(r):
                cols = slice(r * ROUND_COLS, (r + 1) * ROUND_COLS)
                nc.vector.quantize_mx(
                    out=silu_codes[:, cols].bitcast(FP8X4),
                    scales=silu_scales[:, cols],
                    in_=silu_grouped[r][:].rearrange("p c t -> p (c t)"),
                )

            def weights_transpose(w):
                words = w_raw[w][:].bitcast(F32)
                for half in range(2):
                    if w == EXPANDED:
                        wt = psum_wt.tile([P, PACK, 2 * P], BF16, name="wt")
                        for o_local in range(2):
                            for t in range(PACK):
                                first = (2 * half + o_local) * K_PASS + t * P
                                nc.tensor.transpose(
                                    wt[:, t, o_local * P : (o_local + 1) * P], w_raw[w][:, first : first + P], ident_bf16[:]
                                )
                    else:
                        wt = psum_wt.tile([P, 2, 2 * P], F32, name="wt")
                        for o_local in range(2):
                            first = (2 * half + o_local) * (K_PASS // 2)
                            for u in range(2):
                                nc.tensor.transpose(
                                    wt[:, u, o_local * P : (o_local + 1) * P],
                                    words[:, first + u : first + K_PASS // 2 : 2],
                                    ident[:],
                                )
                    transposed[(w, half)] = wt

            def weights_copy(w):
                w_grouped[w] = w_grouped_pool.tile([P, OUT_F * PACK], BF16, name="w_grouped", align_bytes=64)
                for half in range(2):
                    if w == EXPANDED:
                        target, step = w_grouped[w][:, half * 8 * P : (half + 1) * 8 * P], PACK
                    else:
                        target, step = w_grouped[w][:].bitcast(F32)[:, half * 4 * P : (half + 1) * 4 * P], 2
                    nc.scalar.copy(
                        out=target.rearrange("p (o u) -> p o u", u=step),
                        in_=transposed[(w, half)][:].rearrange("p u o -> p o u"),
                    )

            def weights_quantise(w):
                nc.vector.quantize_mx(out=w_codes[:, w, :].bitcast(FP8X4), scales=w_scales[:, w, :], in_=w_grouped[w][:])

            def place(s):
                r, pos = divmod(s, SPLINE_PASSES)
                return r, ORDERS[r][pos]

            def x_rows(s):
                r, g = place(s)
                return x_twice[r][g // PASSES_PER_LOAD][:, g % PASSES_PER_LOAD, :]

            def on_vector(r, g):
                return g != EXPANDED and not squared_on_scalar(r, g)

            def shift(s):
                r, g = place(s)
                h = g // PASSES_PER_LOAD
                if not on_vector(r, g) or (r, h) in shifted:
                    return
                used = [k for k in range(PASSES_PER_LOAD) if on_vector(r, h * PASSES_PER_LOAD + k)]
                shifted[(r, h)] = shifted_pool.tile([P, 2, PASSES_PER_LOAD, ROUND_COLS], F32, name="shifted")
                for u in range(2):
                    nc.vector.tensor_scalar(
                        out=shifted[(r, h)][:, u, used[0] : used[-1] + 1, :],
                        in0=x_twice[r][h][:, used[0] : used[-1] + 1, :],
                        scalar1=3.5,
                        scalar2=pair_mid[:, u : u + 1],
                        op0=ALU.mult,
                        op1=ALU.subtract,
                    )

            def square(s):
                r, g = place(s)
                if g == EXPANDED:
                    product[s] = product_pool.tile([P, PACK * P], F32, name="product")
                    rows = x_chunks[r][:].rearrange("p t c -> p (t c)")
                    nc.vector.scalar_tensor_tensor(
                        out=product[s][:], in0=rows, scalar=row_shift[:], in1=rows, op0=ALU.add, op1=ALU.mult
                    )
                    return
                arg[s] = arg_pool.tile([P, PACK, ROUND_COLS], F32, name="arg")
                if squared_on_scalar(r, g):
                    for t in range(PACK):
                        nc.scalar.activation(
                            out=arg[s][:, t, :], in_=x_rows(s), func=ACT.Square, bias=neg_centre[:, t : t + 1], scale=3.5
                        )
                else:
                    arg_by_e = arg[s][:].rearrange("p (u e) c -> p e u c", e=2)
                    factor = shifted[(r, g // PASSES_PER_LOAD)][:, :, g % PASSES_PER_LOAD, :]
                    for e in range(2):
                        nc.vector.scalar_tensor_tensor(
                            out=arg_by_e[:, e, :, :],
                            in0=factor,
                            scalar=2.0 * e - 1.0,
                            in1=factor,
                            op0=ALU.subtract,
                            op1=ALU.mult,
                        )

            def expand_products(s):
                for j in range(M_TILES):
                    exponents[(s, j)] = psum_wt.tile([P, PACK * P], F32, name="wt")
                    nc.tensor.matmul(exponents[(s, j)][:], lhsT=expand[:, j, :], rhs=product[s][:], start=True, stop=True)

            def exponential(s):
                r, g = place(s)
                grouped[s] = grouped_pool.tile([P, ROUND_COLS, PACK], BF16, name="grouped", align_bytes=64)
                if g == EXPANDED:
                    for j in range(M_TILES):
                        nc.scalar.activation(
                            out=grouped[s][:, j * P : (j + 1) * P, :].rearrange("p (c i) t -> p c t i", i=RUN),
                            in_=exponents[(s, j)][:].rearrange("p (t c i) -> p c t i", t=PACK, i=RUN),
                            func=ACT.Exp,
                            bias=neg_square[:],
                            scale=-1.0,
                        )
                    return
                nc.scalar.activation(
                    out=grouped[s][:].rearrange("p (c i) t -> p c t i", i=RUN),
                    in_=arg[s][:].rearrange("p t (c i) -> p c t i", i=RUN),
                    func=ACT.Exp,
                    bias=0.0 if squared_on_scalar(r, g) else -0.25,
                    scale=-1.0,
                )

            def exponential_tile(s, j):
                r, g = place(s)
                if j == 0:
                    grouped[s] = grouped_pool.tile([P, ROUND_COLS, PACK], BF16, name="grouped", align_bytes=64)
                nc.scalar.activation(
                    out=grouped[s][:, j * P : (j + 1) * P, :].rearrange("p (c i) t -> p c t i", i=RUN),
                    in_=arg[s][:, :, j * P : (j + 1) * P].rearrange("p t (c i) -> p c t i", i=RUN),
                    func=ACT.Exp,
                    bias=0.0 if squared_on_scalar(r, g) else -0.25,
                    scale=-1.0,
                )

            def quantise_tile(s, j):
                if j == 0:
                    codes = operand_pool.tile([P, ROUND_COLS], U32, name="codes", align_bytes=64)
                    scales = operand_pool.tile([P, ROUND_COLS], U8, name="scales", align_bytes=64)
                    operand[s] = (codes, scales)
                codes, scales = operand[s]
                nc.vector.quantize_mx(
                    out=codes[:, j * P : (j + 1) * P].bitcast(FP8X4),
                    scales=scales[:, j * P : (j + 1) * P],
                    in_=grouped[s][:, j * P : (j + 1) * P, :].rearrange("p c t -> p (c t)"),
                )

            def quantise(s):
                codes = operand_pool.tile([P, ROUND_COLS], U32, name="codes", align_bytes=64)
                scales = operand_pool.tile([P, ROUND_COLS], U8, name="scales", align_bytes=64)
                nc.vector.quantize_mx(
                    out=codes[:].bitcast(FP8X4), scales=scales[:], in_=grouped[s][:].rearrange("p c t -> p (c t)")
                )
                operand[s] = (codes, scales)

            def multiply(s, tiles=range(M_TILES)):
                r, g = place(s)
                if s % SPLINE_PASSES == 0:
                    for j in range(M_TILES):
                        acc[j] = psum_acc.tile([P, OUT_F], F32, name="acc")
                        m_cols = slice(r * ROUND_COLS + j * P, r * ROUND_COLS + (j + 1) * P)
                        nc.tensor.matmul_mx(
                            out=acc[j][:],
                            lhsT=silu_codes[:, m_cols].bitcast(FP8X4),
                            lhsT_scale=silu_scales[:, m_cols],
                            rhs=w_codes[:, BASE, :].bitcast(FP8X4),
                            rhs_scale=w_scales[:, BASE, :],
                            start=True,
                            stop=False,
                        )
                codes, scales = operand[s]
                for j in tiles:
                    m_cols = slice(j * P, (j + 1) * P)
                    nc.tensor.matmul_mx(
                        out=acc[j][:],
                        lhsT=codes[:, m_cols].bitcast(FP8X4),
                        lhsT_scale=scales[:, m_cols],
                        rhs=w_codes[:, g, :].bitcast(FP8X4),
                        rhs_scale=w_scales[:, g, :],
                        start=False,
                        stop=(s % SPLINE_PASSES == SPLINE_PASSES - 1),
                    )

            def finish_round(r, tiles=range(M_TILES)):
                for j in tiles:
                    result = result_pool.tile([P, OUT_F], F32, name="result")
                    nc.vector.tensor_tensor(out=result[:], in0=acc[j][:], in1=bias_rows[:], op=ALU.add)
                    first_row = r * ROUND_COLS + j * P
                    nc.sync.dma_start(out=out_rows[first_row : first_row + P, :], in_=result[:])

            shift(0)
            shift(1)
            square(0)
            weights_transpose(BASE)
            weights_transpose(0)
            silu_activation(0)
            weights_copy(BASE)
            silu_activation(1)
            silu_activation(2)
            for ahead in range(1, LEAD):
                shift(ahead + 1)
                square(ahead)
        for i in range(0, STEPS):
            done = i - 1
            if done >= 0:
                quantise(done)
                if done < SPLINE_PASSES:
                    weights_quantise(done)
                if done >= SPLINE_PASSES and done % SPLINE_PASSES == 0:
                    finish_round(done // SPLINE_PASSES - 1)
                multiply(done)
            ahead = i + LEAD
            if ahead + 1 < STEPS:
                shift(ahead + 1)
            if ahead < STEPS:
                square(ahead)
            if i == 0:
                for r in range(ROUNDS):
                    silu_quantise(r)
                weights_quantise(BASE)
            if 0 <= i < SPLINE_PASSES:
                if i + 1 < SPLINE_PASSES:
                    weights_transpose(i + 1)
                weights_copy(i)
            for s in range(i + 1, min(i + LEAD + 1, STEPS)):
                r, g = place(s)
                if g == EXPANDED and s == i + EXPAND_LEAD[r]:
                    expand_products(s)
            if i < STEPS - 1:
                exponential(i)
        last = STEPS - 1
        for j in range(M_TILES):
            exponential_tile(last, j)
        for j in range(M_TILES):
            quantise_tile(last, j)
            multiply(last, (j,))
            if j > 0:
                finish_round(ROUNDS - 1, (j - 1,))
        finish_round(ROUNDS - 1, (M_TILES - 1,))
